import numpy as np
import ml_dtypes


def mxq(x, axis, fmt="e4m3"):
    dtype, down = {"e4m3": (ml_dtypes.float8_e4m3fn, 7), "e5m2": (ml_dtypes.float8_e5m2, 14)}[fmt]
    v = np.moveaxis(np.asarray(x, np.float32).astype(ml_dtypes.bfloat16).astype(np.float64), axis, -1)
    blocks = v.reshape(v.shape[:-1] + (-1, 32))
    amax = np.abs(blocks).max(-1, keepdims=True)
    byte = np.maximum(np.where(amax > 0, np.frexp(amax)[1] - 1 + 127, 0) - down, 1)
    scale = np.exp2(byte - 127.0)
    codes = (blocks / scale).astype(np.float32).astype(dtype).astype(np.float64)
    return np.moveaxis((codes * scale).reshape(v.shape), -1, axis)


WIDE = False


def mx_kscale(k):
    if not WIDE:
        return np.ones(k)
    levels = np.array([20, -20, 10, -10, 0])
    a = np.random.permutation(np.resize(levels, k // 512 * 4)).reshape(k // 512, 4)
    idx = np.arange(k)
    return np.exp2(a[idx // 512, idx % 128 // 32])


BF16 = ml_dtypes.bfloat16


def bf(x):
    return np.asarray(x, np.float32).astype(BF16)


def f64(x):
    return np.asarray(x).astype(np.float64)


B, D, C, P, R = 2048, 1024, 512, 4, 4
EPS = 1e-8
EVERY = 8
GSCALE = 4096.0


def rows(n, u, small):
    g = np.random.standard_normal((n, R))
    v = np.random.standard_normal((n, D))
    for r in range(R):
        v += g[:, r:r + 1] * u[r] / np.sqrt(R)
    if small:
        v[::EVERY] *= 0.5 * EPS / np.linalg.norm(v[::EVERY], axis=1, keepdims=True)
    return v


def setup_inputs():
    sc = mx_kscale(C * P)[::P]
    sk = np.repeat(sc, P)
    u = np.random.standard_normal((R, D))
    x = bf(rows(B, u, False))
    w0 = bf(rows(C * P, u, True))
    g = bf(np.random.standard_normal((B, C)) * np.exp2(np.random.randint(-12, 1, (B, 1))) * GSCALE * sc[None, :])
    xf, wf = f64(x), f64(w0)
    rw = 1.0 / np.maximum(np.linalg.norm(wf, axis=1), EPS)
    xn = xf / np.maximum(np.linalg.norm(xf, axis=1, keepdims=True), EPS)
    sims = xn @ (wf * rw[:, None]).T
    weights = bf(wf / sk[:, None]).reshape(C, P * D)
    return {"x": x, "weights": weights, "sims": np.asarray(sims, np.float32), "w_rnorm": np.asarray(rw, np.float32), "grad_out": g}


def reference(x, weights, sims, w_rnorm, grad_out):
    x = f64(x)
    w = f64(weights).reshape(C * P, D)
    spc = f64(sims).reshape(B, C, P)
    e = np.exp(spc - spc.max(axis=2, keepdims=True))
    scores = e / e.sum(axis=2, keepdims=True)
    pooled = np.sum(scores * spc, axis=2, keepdims=True)
    dsims = (f64(grad_out)[:, :, None] * (scores * (1.0 + spc - pooled))).reshape(B, C * P)
    wn = w * f64(w_rnorm)[:, None]
    dxn = mxq(dsims, 1, "e5m2") @ mxq(wn, 0, "e4m3")
    nx = np.linalg.norm(x, axis=1, keepdims=True)
    xn = x / nx
    return (dxn - xn * np.sum(xn * dxn, axis=1, keepdims=True)) / nx

@@ -1,0 +1,264 @@
+from contextlib import ExitStack
+
+import concourse.mybir as mybir
+from concourse.masks import make_identity
+
+F32 = mybir.dt.float32
+BF16 = mybir.dt.bfloat16
+U32 = mybir.dt.uint32
+U8 = mybir.dt.uint8
+E4M3X4 = mybir.dt.float8_e4m3fn_x4
+E5M2X4 = mybir.dt.float8_e5m2_x4
+ALU = mybir.AluOpType
+ACT = mybir.ActivationFunctionType
+AXIS = mybir.AxisListType
+
+P = 128
+TOKENS = 2048
+FEATURES = 1024
+CLASSES = 512
+PROXIES = 4
+TOKEN_TILES = TOKENS // P
+CLASS_TILES = CLASSES // P
+N_MOVING = 512
+FEATURE_HALVES = FEATURES // N_MOVING
+MX_LAG = 4
+STEPS = TOKEN_TILES + MX_LAG + 1
+
+FLOPS = 2 * TOKENS * CLASSES * PROXIES * FEATURES
+
+
+def tile_lsc_t_v_kernel(tc, x, weights, sims, w_rnorm, grad_out, out):
+    nc = tc.nc
+    with ExitStack() as ctx:
+        ctx.enter_context(tc.manual_schedule())
+        consts = ctx.enter_context(tc.tile_pool(name="consts", bufs=1))
+        wprep = ctx.enter_context(tc.tile_pool(name="wprep", bufs=2))
+        loads = ctx.enter_context(tc.tile_pool(name="loads", bufs=4))
+        big = ctx.enter_context(tc.tile_pool(name="big", bufs=2))
+        perclass = ctx.enter_context(tc.tile_pool(name="perclass", bufs=2))
+        held = ctx.enter_context(tc.tile_pool(name="held", bufs=MX_LAG + 3))
+        outs = ctx.enter_context(tc.tile_pool(name="outs", bufs=2))
+        psum_t = ctx.enter_context(tc.psum_pool(name="psum_t", bufs=3))
+        psum_1 = ctx.enter_context(tc.psum_pool(name="psum_1", bufs=1))
+
+        ident = consts.tile([P, P], F32)
+        make_identity(nc, ident[:])
+        rnorm = consts.tile([P, CLASS_TILES, PROXIES], F32)
+        w_codes = consts.tile([P, CLASS_TILES, FEATURES], U32, align_bytes=64)
+        w_scales = consts.tile([P, CLASS_TILES, FEATURES], U8, align_bytes=64)
+
+        tiles = {}
+
+        def valid(i):
+            return 0 <= i < TOKEN_TILES
+
+        def load_inputs(i):
+            rows = slice(i * P, (i + 1) * P)
+            s_sb = loads.tile([P, CLASSES * PROXIES], F32)
+            nc.sync.dma_start(out=s_sb[:], in_=sims[rows, :])
+            x_sb = held.tile([P, FEATURES], BF16, bufs=MX_LAG + 4)
+            nc.sync.dma_start(out=x_sb[:], in_=x[rows, :])
+            g_sb = loads.tile([P, CLASSES], BF16)
+            nc.sync.dma_start(out=g_sb[:], in_=grad_out[rows, :])
+            tiles["s", i], tiles["x", i], tiles["g", i] = s_sb, x_sb, g_sb
+
+        def load_weights(u):
+            raw = wprep.tile([P, PROXIES, FEATURES], BF16)
+            nc.sync.dma_start(
+                out=raw[:],
+                in_=weights[u * P : (u + 1) * P, :].rearrange("c (p d) -> c p d", p=PROXIES),
+            )
+            tiles["raw", u] = raw
+
+        def prepare_wn(u):
+            grouped = wprep.tile([P, FEATURES, PROXIES], BF16, align_bytes=64)
+            nc.gpsimd.tensor_tensor(
+                out=grouped[:], in0=tiles["raw", u][:].rearrange("c p d -> c d p"),
+                in1=rnorm[:, u, :].unsqueeze(1).to_broadcast([P, FEATURES, PROXIES]),
+                op=ALU.mult,
+            )
+            nc.vector.quantize_mx(
+                out=w_codes[:, u, :].bitcast(E4M3X4), scales=w_scales[:, u, :],
+                in_=grouped[:].rearrange("c d p -> c (d p)"),
+            )
+
+        def neg_max(i):
+            neg_m = perclass.tile([P, CLASSES], F32, bufs=3)
+            nc.vector.tensor_reduce(
+                out=neg_m[:], in_=tiles["s", i][:].rearrange("b (c p) -> b c p", p=PROXIES),
+                axis=AXIS.X, op=ALU.max, negate=True,
+            )
+            tiles["neg_m", i] = neg_m
+
+        def transpose_plus(i, u, addend):
+            bank = psum_t.tile([P, PROXIES, P], F32)
+            by_proxy = tiles["s", i][:].rearrange("b (u c p) -> b u p c", u=CLASS_TILES, p=PROXIES)
+            for p in range(PROXIES):
+                nc.tensor.matmul(
+                    out=bank[:, p, :], lhsT=by_proxy[:, u, p, :], rhs=ident[:],
+                    is_transpose=True, start=True, stop=False,
+                )
+                nc.tensor.matmul(
+                    out=bank[:, p, :], lhsT=addend[:, u * P : (u + 1) * P], rhs=ident[:],
+                    is_transpose=True, start=False, stop=True,
+                )
+            return bank
+
+        def exponentials(i):
+            e = big.tile([P, CLASS_TILES, PROXIES, P], F32, bufs=3)
+            ed = big.tile([P, CLASS_TILES, PROXIES, P], F32)
+            tiles["e", i], tiles["ed", i] = e, ed
+            d_t = [transpose_plus(i, u, tiles["neg_m", i]) for u in range(CLASS_TILES)]
+            for u in range(CLASS_TILES):
+                nc.scalar.activation(out=e[:, u], in_=d_t[u][:], func=ACT.Exp)
+                nc.vector.tensor_tensor(out=ed[:, u], in0=d_t[u][:], in1=e[:, u], op=ALU.mult)
+            nx2 = held.tile([P, 1], F32)
+            x_sq = outs.tile([P, FEATURES], BF16, bufs=1)
+            nc.scalar.activation(
+                out=x_sq[:], in_=tiles["x", i][:], func=ACT.Square, accum_out=nx2[:]
+            )
+            tiles["nx2", i] = nx2
+
+        def proxy_sums(i):
+            z_u = psum_1.tile([P, CLASSES], F32)
+            n_u = psum_1.tile([P, CLASSES], F32)
+            for u in range(CLASS_TILES):
+                for src, dst in ((tiles["e", i], z_u), (tiles["ed", i], n_u)):
+                    for p in range(PROXIES):
+                        nc.tensor.matmul(
+                            out=dst[:, u * P : (u + 1) * P], lhsT=src[:, u, p, :], rhs=ident[:],
+                            is_transpose=True, start=(p == 0), stop=(p == PROXIES - 1),
+                        )
+            tiles["z", i], tiles["n", i] = z_u, n_u
+
+        def reciprocals(i):
+            ln_z = perclass.tile([P, CLASSES], F32, bufs=1)
+            nc.scalar.activation(out=ln_z[:], in_=tiles["z", i][:], func=ACT.Ln)
+            ln_nx2 = held.tile([P, 1], F32)
+            nc.scalar.activation(out=ln_nx2[:], in_=tiles["nx2", i][:], func=ACT.Ln)
+            rz = perclass.tile([P, CLASSES], F32)
+            nc.scalar.activation(out=rz[:], in_=ln_z[:], func=ACT.Exp, scale=-1.0)
+            inv_nx = held.tile([P, 1], F32)
+            nc.scalar.activation(out=inv_nx[:], in_=ln_nx2[:], func=ACT.Exp, scale=-0.5)
+            inv_nx3 = held.tile([P, 1], F32)
+            nc.scalar.activation(out=inv_nx3[:], in_=ln_nx2[:], func=ACT.Exp, scale=-1.5)
+            tiles["rz", i], tiles["inv_nx", i], tiles["inv_nx3", i] = rz, inv_nx, inv_nx3
+
+        def per_class(i):
+            q = perclass.tile([P, CLASSES], F32)
+            nc.vector.tensor_tensor(out=q[:], in0=tiles["n", i][:], in1=tiles["rz", i][:], op=ALU.mult)
+            neg_pooled = perclass.tile([P, CLASSES], F32)
+            nc.gpsimd.tensor_tensor(
+                out=neg_pooled[:], in0=tiles["neg_m", i][:], in1=q[:], op=ALU.subtract
+            )
+            g_rz = perclass.tile([P, CLASSES], F32)
+            nc.gpsimd.tensor_tensor(
+                out=g_rz[:], in0=tiles["g", i][:], in1=tiles["rz", i][:], op=ALU.mult
+            )
+            tiles["neg_pooled", i], tiles["g_rz", i] = neg_pooled, g_rz
+
+        def gradient(i):
+            e = tiles["e", i]
+            r = big.tile([P, CLASS_TILES, PROXIES, P], F32)
+            for u in range(CLASS_TILES):
+                h_t = transpose_plus(i, u, tiles["neg_pooled", i])
+                nc.vector.scalar_tensor_tensor(
+                    out=r[:, u], in0=h_t[:], scalar=1.0, in1=e[:, u], op0=ALU.add, op1=ALU.mult
+                )
+            a_t = psum_1.tile([P, CLASS_TILES, P], F32)
+            for u in range(CLASS_TILES):
+                nc.tensor.transpose(a_t[:, u, :], tiles["g_rz", i][:, u * P : (u + 1) * P], ident[:])
+            dsims = big.tile([P, CLASS_TILES, P, PROXIES], BF16, align_bytes=64)
+            nc.vector.tensor_tensor(
+                out=dsims[:], in0=r[:].rearrange("c u p b -> c u b p"),
+                in1=a_t[:].unsqueeze(3).to_broadcast([P, CLASS_TILES, P, PROXIES]), op=ALU.mult,
+            )
+            d_codes = held.tile([P, CLASS_TILES * P], U32, align_bytes=64)
+            d_scales = held.tile([P, CLASS_TILES * P], U8, align_bytes=64)
+            nc.vector.quantize_mx(
+                out=d_codes[:].bitcast(E5M2X4), scales=d_scales[:],
+                in_=dsims[:].rearrange("c u b p -> c (u b p)"),
+            )
+            tiles["codes", i], tiles["scales", i] = d_codes, d_scales
+
+        def mx_matmuls(i):
+            d_codes, d_scales = tiles["codes", i], tiles["scales", i]
+            for half in range(FEATURE_HALVES):
+                cols = slice(half * N_MOVING, (half + 1) * N_MOVING)
+                acc = psum_1.tile([P, N_MOVING], F32, name="acc%d" % half)
+                tiles["acc%d" % half, i] = acc
+                for u in range(CLASS_TILES):
+                    toks = slice(u * P, (u + 1) * P)
+                    nc.tensor.matmul_mx(
+                        out=acc[:],
+                        lhsT=d_codes[:, toks].bitcast(E5M2X4), lhsT_scale=d_scales[:, toks],
+                        rhs=w_codes[:, u, cols].bitcast(E4M3X4), rhs_scale=w_scales[:, u, cols],
+                        start=(u == 0), stop=(u == CLASS_TILES - 1),
+                    )
+
+        def leave_psum(i):
+            y = outs.tile([P, FEATURES], F32, bufs=3)
+            dots = outs.tile([P, FEATURE_HALVES], F32)
+            for half in range(FEATURE_HALVES):
+                cols = slice(half * N_MOVING, (half + 1) * N_MOVING)
+                acc = tiles["acc%d" % half, i]
+                nc.scalar.activation(
+                    out=y[:, cols], in_=acc[:], func=ACT.Copy, scale=tiles["inv_nx", i][:, 0:1]
+                )
+                products = outs.tile([P, N_MOVING], F32)
+                nc.vector.scalar_tensor_tensor(
+                    out=products[:], in0=acc[:], scalar=1.0, in1=tiles["x", i][:, cols],
+                    op0=ALU.mult, op1=ALU.mult, accum_out=dots[:, half : half + 1],
+                )
+            coef = outs.tile([P, 1], F32)
+            nc.vector.tensor_scalar(
+                out=coef[:], in0=dots[:, 0:1], scalar1=dots[:, 1:2],
+                scalar2=tiles["inv_nx3", i][:, 0:1], op0=ALU.add, op1=ALU.mult,
+            )
+            neg_coef = outs.tile([P, 1], F32)
+            nc.vector.tensor_scalar(
+                out=neg_coef[:], in0=coef[:], scalar1=-1.0, scalar2=None, op0=ALU.mult
+            )
+            tiles["y", i], tiles["neg_coef", i] = y, neg_coef
+
+        def project_and_store(i):
+            y = tiles["y", i]
+            nc.vector.scalar_tensor_tensor(
+                out=y[:], in0=tiles["x", i][:], scalar=tiles["neg_coef", i][:, 0:1], in1=y[:],
+                op0=ALU.mult, op1=ALU.add,
+            )
+            nc.sync.dma_start(out=out[i * P : (i + 1) * P, :], in_=y[:])
+
+        load_inputs(0)
+        nc.sync.dma_start(
+            out=rnorm[:], in_=w_rnorm.rearrange("(u c p) -> c u p", u=CLASS_TILES, p=PROXIES)
+        )
+        load_weights(0)
+        load_inputs(1)
+        neg_max(0)
+        for step in range(STEPS):
+            if valid(step + 2):
+                load_inputs(step + 2)
+            if step + 1 < CLASS_TILES:
+                load_weights(step + 1)
+            if valid(step):
+                exponentials(step)
+            if valid(step - MX_LAG - 1):
+                leave_psum(step - MX_LAG - 1)
+            if valid(step):
+                proxy_sums(step)
+            if valid(step + 1):
+                neg_max(step + 1)
+            if valid(step - 1):
+                gradient(step - 1)
+            if valid(step - MX_LAG):
+                mx_matmuls(step - MX_LAG)
+            if valid(step):
+                reciprocals(step)
+            if step < CLASS_TILES:
+                prepare_wn(step)
+            if valid(step):
+                per_class(step)
+            if valid(step - MX_LAG - 1):
+                project_and_store(step - MX_LAG - 1)

@@ -23,7 +23,7 @@ CLASS_TILES = CLASSES // P
 N_MOVING = 512
 FEATURE_HALVES = FEATURES // N_MOVING
 MX_LAG = 4
-STEPS = TOKEN_TILES + MX_LAG + 1
+STEPS = TOKEN_TILES + MX_LAG
 
 FLOPS = 2 * TOKENS * CLASSES * PROXIES * FEATURES
 
@@ -33,8 +33,8 @@ def tile_lsc_t_v_kernel(tc, x, weights, sims, w_rnorm, grad_out, out):
     with ExitStack() as ctx:
         ctx.enter_context(tc.manual_schedule())
         consts = ctx.enter_context(tc.tile_pool(name="consts", bufs=1))
-        wprep = ctx.enter_context(tc.tile_pool(name="wprep", bufs=2))
-        loads = ctx.enter_context(tc.tile_pool(name="loads", bufs=4))
+        wprep = ctx.enter_context(tc.tile_pool(name="wprep", bufs=1))
+        loads = ctx.enter_context(tc.tile_pool(name="loads", bufs=3))
         big = ctx.enter_context(tc.tile_pool(name="big", bufs=2))
         perclass = ctx.enter_context(tc.tile_pool(name="perclass", bufs=2))
         held = ctx.enter_context(tc.tile_pool(name="held", bufs=MX_LAG + 3))
@@ -64,7 +64,7 @@ def tile_lsc_t_v_kernel(tc, x, weights, sims, w_rnorm, grad_out, out):
             tiles["s", i], tiles["x", i], tiles["g", i] = s_sb, x_sb, g_sb
 
         def load_weights(u):
-            raw = wprep.tile([P, PROXIES, FEATURES], BF16)
+            raw = wprep.tile([P, PROXIES, FEATURES], BF16, bufs=2)
             nc.sync.dma_start(
                 out=raw[:],
                 in_=weights[u * P : (u + 1) * P, :].rearrange("c (p d) -> c p d", p=PROXIES),
@@ -72,47 +72,54 @@ def tile_lsc_t_v_kernel(tc, x, weights, sims, w_rnorm, grad_out, out):
             tiles["raw", u] = raw
 
         def prepare_wn(u):
+            scaled = wprep.tile([P, PROXIES, FEATURES], BF16)
+            for p in range(PROXIES):
+                nc.scalar.activation(
+                    out=scaled[:, p, :], in_=tiles["raw", u][:, p, :], func=ACT.Copy,
+                    scale=rnorm[:, u, p : p + 1],
+                )
             grouped = wprep.tile([P, FEATURES, PROXIES], BF16, align_bytes=64)
-            nc.gpsimd.tensor_tensor(
-                out=grouped[:], in0=tiles["raw", u][:].rearrange("c p d -> c d p"),
-                in1=rnorm[:, u, :].unsqueeze(1).to_broadcast([P, FEATURES, PROXIES]),
-                op=ALU.mult,
+            nc.vector.tensor_copy(
+                out=grouped[:].rearrange("c (n i) p -> c n p i", i=4),
+                in_=scaled[:].rearrange("c p (n i) -> c n p i", i=4),
             )
             nc.vector.quantize_mx(
                 out=w_codes[:, u, :].bitcast(E4M3X4), scales=w_scales[:, u, :],
                 in_=grouped[:].rearrange("c d p -> c (d p)"),
             )
 
-        def neg_max(i):
-            neg_m = perclass.tile([P, CLASSES], F32, bufs=3)
+        def shift_by_max(i):
+            neg_m = perclass.tile([P, CLASSES], F32)
             nc.vector.tensor_reduce(
                 out=neg_m[:], in_=tiles["s", i][:].rearrange("b (c p) -> b c p", p=PROXIES),
                 axis=AXIS.X, op=ALU.max, negate=True,
             )
-            tiles["neg_m", i] = neg_m
+            planes = big.tile([P, PROXIES, CLASSES], F32, bufs=3)
+            nc.gpsimd.tensor_tensor(
+                out=planes[:], in0=tiles["s", i][:].rearrange("b (c p) -> b p c", p=PROXIES),
+                in1=neg_m[:].unsqueeze(1).to_broadcast([P, PROXIES, CLASSES]), op=ALU.add,
+            )
+            tiles["planes", i] = planes
 
-        def transpose_plus(i, u, addend):
+        def transpose_planes(i, u):
             bank = psum_t.tile([P, PROXIES, P], F32)
-            by_proxy = tiles["s", i][:].rearrange("b (u c p) -> b u p c", u=CLASS_TILES, p=PROXIES)
             for p in range(PROXIES):
-                nc.tensor.matmul(
-                    out=bank[:, p, :], lhsT=by_proxy[:, u, p, :], rhs=ident[:],
-                    is_transpose=True, start=True, stop=False,
-                )
-                nc.tensor.matmul(
-                    out=bank[:, p, :], lhsT=addend[:, u * P : (u + 1) * P], rhs=ident[:],
-                    is_transpose=True, start=False, stop=True,
+                nc.tensor.transpose(
+                    bank[:, p, :], tiles["planes", i][:, p, u * P : (u + 1) * P], ident[:]
                 )
             return bank
 
+        def transpose_shifted(i):
+            tiles["d_t", i] = [transpose_planes(i, u) for u in range(CLASS_TILES)]
+
         def exponentials(i):
-            e = big.tile([P, CLASS_TILES, PROXIES, P], F32, bufs=3)
+            e = big.tile([P, CLASS_TILES, PROXIES, P], F32)
             ed = big.tile([P, CLASS_TILES, PROXIES, P], F32)
             tiles["e", i], tiles["ed", i] = e, ed
-            d_t = [transpose_plus(i, u, tiles["neg_m", i]) for u in range(CLASS_TILES)]
             for u in range(CLASS_TILES):
-                nc.scalar.activation(out=e[:, u], in_=d_t[u][:], func=ACT.Exp)
-                nc.vector.tensor_tensor(out=ed[:, u], in0=d_t[u][:], in1=e[:, u], op=ALU.mult)
+                d_t = tiles["d_t", i][u]
+                nc.scalar.activation(out=e[:, u], in_=d_t[:], func=ACT.Exp)
+                nc.vector.tensor_tensor(out=ed[:, u], in0=d_t[:], in1=e[:, u], op=ALU.mult)
             nx2 = held.tile([P, 1], F32)
             x_sq = outs.tile([P, FEATURES], BF16, bufs=1)
             nc.scalar.activation(
@@ -120,17 +127,17 @@ def tile_lsc_t_v_kernel(tc, x, weights, sims, w_rnorm, grad_out, out):
             )
             tiles["nx2", i] = nx2
 
-        def proxy_sums(i):
-            z_u = psum_1.tile([P, CLASSES], F32)
-            n_u = psum_1.tile([P, CLASSES], F32)
-            for u in range(CLASS_TILES):
-                for src, dst in ((tiles["e", i], z_u), (tiles["ed", i], n_u)):
-                    for p in range(PROXIES):
-                        nc.tensor.matmul(
-                            out=dst[:, u * P : (u + 1) * P], lhsT=src[:, u, p, :], rhs=ident[:],
-                            is_transpose=True, start=(p == 0), stop=(p == PROXIES - 1),
-                        )
-            tiles["z", i], tiles["n", i] = z_u, n_u
+        def open_proxy_sums(i):
+            tiles["z", i] = psum_1.tile([P, CLASSES], F32, name="z_u")
+            tiles["n", i] = psum_1.tile([P, CLASSES], F32, name="n_u")
+
+        def proxy_sums(i, u):
+            for src, dst in ((tiles["e", i], tiles["z", i]), (tiles["ed", i], tiles["n", i])):
+                for p in range(PROXIES):
+                    nc.tensor.matmul(
+                        out=dst[:, u * P : (u + 1) * P], lhsT=src[:, u, p, :], rhs=ident[:],
+                        is_transpose=True, start=(p == 0), stop=(p == PROXIES - 1),
+                    )
 
         def reciprocals(i):
             ln_z = perclass.tile([P, CLASSES], F32, bufs=1)
@@ -148,21 +155,22 @@ def tile_lsc_t_v_kernel(tc, x, weights, sims, w_rnorm, grad_out, out):
         def per_class(i):
             q = perclass.tile([P, CLASSES], F32)
             nc.vector.tensor_tensor(out=q[:], in0=tiles["n", i][:], in1=tiles["rz", i][:], op=ALU.mult)
-            neg_pooled = perclass.tile([P, CLASSES], F32)
-            nc.gpsimd.tensor_tensor(
-                out=neg_pooled[:], in0=tiles["neg_m", i][:], in1=q[:], op=ALU.subtract
-            )
             g_rz = perclass.tile([P, CLASSES], F32)
             nc.gpsimd.tensor_tensor(
                 out=g_rz[:], in0=tiles["g", i][:], in1=tiles["rz", i][:], op=ALU.mult
             )
-            tiles["neg_pooled", i], tiles["g_rz", i] = neg_pooled, g_rz
+            tiles["g_rz", i] = g_rz
+            planes = tiles["planes", i]
+            nc.gpsimd.tensor_tensor(
+                out=planes[:], in0=planes[:],
+                in1=q[:].unsqueeze(1).to_broadcast([P, PROXIES, CLASSES]), op=ALU.subtract,
+            )
 
         def gradient(i):
             e = tiles["e", i]
-            r = big.tile([P, CLASS_TILES, PROXIES, P], F32)
+            r = big.tile([P, CLASS_TILES, PROXIES, P], F32, bufs=1)
             for u in range(CLASS_TILES):
-                h_t = transpose_plus(i, u, tiles["neg_pooled", i])
+                h_t = transpose_planes(i, u)
                 nc.vector.scalar_tensor_tensor(
                     out=r[:, u], in0=h_t[:], scalar=1.0, in1=e[:, u], op0=ALU.add, op1=ALU.mult
                 )
@@ -174,43 +182,52 @@ def tile_lsc_t_v_kernel(tc, x, weights, sims, w_rnorm, grad_out, out):
                 out=dsims[:], in0=r[:].rearrange("c u p b -> c u b p"),
                 in1=a_t[:].unsqueeze(3).to_broadcast([P, CLASS_TILES, P, PROXIES]), op=ALU.mult,
             )
-            d_codes = held.tile([P, CLASS_TILES * P], U32, align_bytes=64)
-            d_scales = held.tile([P, CLASS_TILES * P], U8, align_bytes=64)
+            d_codes = held.tile([P, CLASS_TILES * P], U32, bufs=MX_LAG + 1, align_bytes=64)
+            d_scales = held.tile([P, CLASS_TILES * P], U8, bufs=MX_LAG + 1, align_bytes=64)
             nc.vector.quantize_mx(
                 out=d_codes[:].bitcast(E5M2X4), scales=d_scales[:],
                 in_=dsims[:].rearrange("c u b p -> c (u b p)"),
             )
             tiles["codes", i], tiles["scales", i] = d_codes, d_scales
 
-        def mx_matmuls(i):
-            d_codes, d_scales = tiles["codes", i], tiles["scales", i]
-            for half in range(FEATURE_HALVES):
-                cols = slice(half * N_MOVING, (half + 1) * N_MOVING)
-                acc = psum_1.tile([P, N_MOVING], F32, name="acc%d" % half)
-                tiles["acc%d" % half, i] = acc
-                for u in range(CLASS_TILES):
-                    toks = slice(u * P, (u + 1) * P)
-                    nc.tensor.matmul_mx(
-                        out=acc[:],
-                        lhsT=d_codes[:, toks].bitcast(E5M2X4), lhsT_scale=d_scales[:, toks],
-                        rhs=w_codes[:, u, cols].bitcast(E4M3X4), rhs_scale=w_scales[:, u, cols],
-                        start=(u == 0), stop=(u == CLASS_TILES - 1),
-                    )
+        def mx_pair(i, half, first_u):
+            if not valid(i):
+                return
+            if first_u == 0:
+                tiles["acc", i, half] = psum_1.tile([P, N_MOVING], F32, name="acc%d" % half)
+            cols = slice(half * N_MOVING, (half + 1) * N_MOVING)
+            for u in (first_u, first_u + 1):
+                toks = slice(u * P, (u + 1) * P)
+                nc.tensor.matmul_mx(
+                    out=tiles["acc", i, half][:],
+                    lhsT=tiles["codes", i][:, toks].bitcast(E5M2X4),
+                    lhsT_scale=tiles["scales", i][:, toks],
+                    rhs=w_codes[:, u, cols].bitcast(E4M3X4), rhs_scale=w_scales[:, u, cols],
+                    start=(u == 0), stop=(u == CLASS_TILES - 1),
+                )
 
-        def leave_psum(i):
-            y = outs.tile([P, FEATURES], F32, bufs=3)
-            dots = outs.tile([P, FEATURE_HALVES], F32)
-            for half in range(FEATURE_HALVES):
-                cols = slice(half * N_MOVING, (half + 1) * N_MOVING)
-                acc = tiles["acc%d" % half, i]
-                nc.scalar.activation(
-                    out=y[:, cols], in_=acc[:], func=ACT.Copy, scale=tiles["inv_nx", i][:, 0:1]
-                )
-                products = outs.tile([P, N_MOVING], F32)
-                nc.vector.scalar_tensor_tensor(
-                    out=products[:], in0=acc[:], scalar=1.0, in1=tiles["x", i][:, cols],
-                    op0=ALU.mult, op1=ALU.mult, accum_out=dots[:, half : half + 1],
-                )
+        def leave_psum(i, half):
+            if not valid(i):
+                return
+            if half == 0:
+                tiles["y", i] = outs.tile([P, FEATURES], F32, name="y", bufs=3)
+                tiles["dots", i] = outs.tile([P, FEATURE_HALVES], F32, name="dots")
+            cols = slice(half * N_MOVING, (half + 1) * N_MOVING)
+            acc = tiles["acc", i, half]
+            nc.scalar.activation(
+                out=tiles["y", i][:, cols], in_=acc[:], func=ACT.Copy,
+                scale=tiles["inv_nx", i][:, 0:1],
+            )
+            products = outs.tile([P, N_MOVING], F32)
+            nc.vector.scalar_tensor_tensor(
+                out=products[:], in0=acc[:], scalar=1.0, in1=tiles["x", i][:, cols],
+                op0=ALU.mult, op1=ALU.mult, accum_out=tiles["dots", i][:, half : half + 1],
+            )
+
+        def project_and_store(i):
+            if not valid(i):
+                return
+            y, dots = tiles["y", i], tiles["dots", i]
             coef = outs.tile([P, 1], F32)
             nc.vector.tensor_scalar(
                 out=coef[:], in0=dots[:, 0:1], scalar1=dots[:, 1:2],
@@ -220,12 +237,8 @@ def tile_lsc_t_v_kernel(tc, x, weights, sims, w_rnorm, grad_out, out):
             nc.vector.tensor_scalar(
                 out=neg_coef[:], in0=coef[:], scalar1=-1.0, scalar2=None, op0=ALU.mult
             )
-            tiles["y", i], tiles["neg_coef", i] = y, neg_coef
-
-        def project_and_store(i):
-            y = tiles["y", i]
             nc.vector.scalar_tensor_tensor(
-                out=y[:], in0=tiles["x", i][:], scalar=tiles["neg_coef", i][:, 0:1], in1=y[:],
+                out=y[:], in0=tiles["x", i][:], scalar=neg_coef[:, 0:1], in1=y[:],
                 op0=ALU.mult, op1=ALU.add,
             )
             nc.sync.dma_start(out=out[i * P : (i + 1) * P, :], in_=y[:])
@@ -236,29 +249,38 @@ def tile_lsc_t_v_kernel(tc, x, weights, sims, w_rnorm, grad_out, out):
         )
         load_weights(0)
         load_inputs(1)
-        neg_max(0)
+        shift_by_max(0)
         for step in range(STEPS):
+            mx_tile = step - MX_LAG
             if valid(step + 2):
                 load_inputs(step + 2)
             if step + 1 < CLASS_TILES:
                 load_weights(step + 1)
             if valid(step):
-                exponentials(step)
-            if valid(step - MX_LAG - 1):
-                leave_psum(step - MX_LAG - 1)
+                transpose_shifted(step)
+            mx_pair(mx_tile, 0, 0)
             if valid(step):
-                proxy_sums(step)
+                exponentials(step)
             if valid(step + 1):
-                neg_max(step + 1)
+                shift_by_max(step + 1)
+            if valid(step):
+                open_proxy_sums(step)
+                proxy_sums(step, 0)
+                proxy_sums(step, 1)
+            mx_pair(mx_tile, 0, 2)
+            if valid(step):
+                proxy_sums(step, 2)
+                proxy_sums(step, 3)
+            mx_pair(mx_tile, 1, 0)
+            leave_psum(mx_tile, 0)
             if valid(step - 1):
                 gradient(step - 1)
-            if valid(step - MX_LAG):
-                mx_matmuls(step - MX_LAG)
+            mx_pair(mx_tile, 1, 2)
             if valid(step):
                 reciprocals(step)
             if step < CLASS_TILES:
                 prepare_wn(step)
             if valid(step):
                 per_class(step)
-            if valid(step - MX_LAG - 1):
-                project_and_store(step - MX_LAG - 1)
+            leave_psum(mx_tile, 1)
+            project_and_store(mx_tile)

@@ -23,7 +23,7 @@ CLASS_TILES = CLASSES // P
 N_MOVING = 512
 FEATURE_HALVES = FEATURES // N_MOVING
 MX_LAG = 4
-STEPS = TOKEN_TILES + MX_LAG
+STEPS = TOKEN_TILES + MX_LAG + 1
 
 FLOPS = 2 * TOKENS * CLASSES * PROXIES * FEATURES
 
@@ -31,7 +31,6 @@ FLOPS = 2 * TOKENS * CLASSES * PROXIES * FEATURES
 def tile_lsc_t_v_kernel(tc, x, weights, sims, w_rnorm, grad_out, out):
     nc = tc.nc
     with ExitStack() as ctx:
-        ctx.enter_context(tc.manual_schedule())
         consts = ctx.enter_context(tc.tile_pool(name="consts", bufs=1))
         wprep = ctx.enter_context(tc.tile_pool(name="wprep", bufs=1))
         loads = ctx.enter_context(tc.tile_pool(name="loads", bufs=3))
@@ -48,6 +47,10 @@ def tile_lsc_t_v_kernel(tc, x, weights, sims, w_rnorm, grad_out, out):
         w_codes = consts.tile([P, CLASS_TILES, FEATURES], U32, align_bytes=64)
         w_scales = consts.tile([P, CLASS_TILES, FEATURES], U8, align_bytes=64)
 
+        exponents = consts.tile([P, 2], F32)
+        nc.gpsimd.memset(exponents[:, 0:1], -0.5)
+        nc.gpsimd.memset(exponents[:, 1:2], -1.5)
+
         tiles = {}
 
         def valid(i):
@@ -57,14 +60,14 @@ def tile_lsc_t_v_kernel(tc, x, weights, sims, w_rnorm, grad_out, out):
             rows = slice(i * P, (i + 1) * P)
             s_sb = loads.tile([P, CLASSES * PROXIES], F32)
             nc.sync.dma_start(out=s_sb[:], in_=sims[rows, :])
-            x_sb = held.tile([P, FEATURES], BF16, bufs=MX_LAG + 4)
+            x_sb = held.tile([P, FEATURES], BF16, bufs=MX_LAG + 5)
             nc.sync.dma_start(out=x_sb[:], in_=x[rows, :])
-            g_sb = loads.tile([P, CLASSES], BF16)
+            g_sb = loads.tile([P, CLASSES], BF16, bufs=4)
             nc.sync.dma_start(out=g_sb[:], in_=grad_out[rows, :])
             tiles["s", i], tiles["x", i], tiles["g", i] = s_sb, x_sb, g_sb
 
         def load_weights(u):
-            raw = wprep.tile([P, PROXIES, FEATURES], BF16, bufs=2)
+            raw = wprep.tile([P, PROXIES, FEATURES], BF16)
             nc.sync.dma_start(
                 out=raw[:],
                 in_=weights[u * P : (u + 1) * P, :].rearrange("c (p d) -> c p d", p=PROXIES),
@@ -89,12 +92,12 @@ def tile_lsc_t_v_kernel(tc, x, weights, sims, w_rnorm, grad_out, out):
             )
 
         def shift_by_max(i):
-            neg_m = perclass.tile([P, CLASSES], F32)
+            neg_m = perclass.tile([P, CLASSES], F32, bufs=1)
             nc.vector.tensor_reduce(
                 out=neg_m[:], in_=tiles["s", i][:].rearrange("b (c p) -> b c p", p=PROXIES),
                 axis=AXIS.X, op=ALU.max, negate=True,
             )
-            planes = big.tile([P, PROXIES, CLASSES], F32, bufs=3)
+            planes = big.tile([P, PROXIES, CLASSES], F32, bufs=4)
             nc.gpsimd.tensor_tensor(
                 out=planes[:], in0=tiles["s", i][:].rearrange("b (c p) -> b p c", p=PROXIES),
                 in1=neg_m[:].unsqueeze(1).to_broadcast([P, PROXIES, CLASSES]), op=ALU.add,
@@ -113,8 +116,8 @@ def tile_lsc_t_v_kernel(tc, x, weights, sims, w_rnorm, grad_out, out):
             tiles["d_t", i] = [transpose_planes(i, u) for u in range(CLASS_TILES)]
 
         def exponentials(i):
-            e = big.tile([P, CLASS_TILES, PROXIES, P], F32)
-            ed = big.tile([P, CLASS_TILES, PROXIES, P], F32)
+            e = big.tile([P, CLASS_TILES, PROXIES, P], F32, bufs=3)
+            ed = big.tile([P, CLASS_TILES, PROXIES, P], F32, bufs=1)
             tiles["e", i], tiles["ed", i] = e, ed
             for u in range(CLASS_TILES):
                 d_t = tiles["d_t", i][u]
@@ -125,7 +128,11 @@ def tile_lsc_t_v_kernel(tc, x, weights, sims, w_rnorm, grad_out, out):
             nc.scalar.activation(
                 out=x_sq[:], in_=tiles["x", i][:], func=ACT.Square, accum_out=nx2[:]
             )
-            tiles["nx2", i] = nx2
+            inv_nx = held.tile([P, 2], F32)
+            nc.gpsimd.tensor_tensor(
+                out=inv_nx[:], in0=nx2[:].to_broadcast([P, 2]), in1=exponents[:], op=ALU.pow
+            )
+            tiles["inv_nx", i] = inv_nx
 
         def open_proxy_sums(i):
             tiles["z", i] = psum_1.tile([P, CLASSES], F32, name="z_u")
@@ -142,29 +149,25 @@ def tile_lsc_t_v_kernel(tc, x, weights, sims, w_rnorm, grad_out, out):
         def reciprocals(i):
             ln_z = perclass.tile([P, CLASSES], F32, bufs=1)
             nc.scalar.activation(out=ln_z[:], in_=tiles["z", i][:], func=ACT.Ln)
-            ln_nx2 = held.tile([P, 1], F32)
-            nc.scalar.activation(out=ln_nx2[:], in_=tiles["nx2", i][:], func=ACT.Ln)
             rz = perclass.tile([P, CLASSES], F32)
             nc.scalar.activation(out=rz[:], in_=ln_z[:], func=ACT.Exp, scale=-1.0)
-            inv_nx = held.tile([P, 1], F32)
-            nc.scalar.activation(out=inv_nx[:], in_=ln_nx2[:], func=ACT.Exp, scale=-0.5)
-            inv_nx3 = held.tile([P, 1], F32)
-            nc.scalar.activation(out=inv_nx3[:], in_=ln_nx2[:], func=ACT.Exp, scale=-1.5)
-            tiles["rz", i], tiles["inv_nx", i], tiles["inv_nx3", i] = rz, inv_nx, inv_nx3
+            tiles["rz", i] = rz
 
         def per_class(i):
             q = perclass.tile([P, CLASSES], F32)
             nc.vector.tensor_tensor(out=q[:], in0=tiles["n", i][:], in1=tiles["rz", i][:], op=ALU.mult)
-            g_rz = perclass.tile([P, CLASSES], F32)
-            nc.gpsimd.tensor_tensor(
-                out=g_rz[:], in0=tiles["g", i][:], in1=tiles["rz", i][:], op=ALU.mult
-            )
-            tiles["g_rz", i] = g_rz
             planes = tiles["planes", i]
             nc.gpsimd.tensor_tensor(
                 out=planes[:], in0=planes[:],
                 in1=q[:].unsqueeze(1).to_broadcast([P, PROXIES, CLASSES]), op=ALU.subtract,
             )
+
+        def scale_grad_out(i):
+            g_rz = perclass.tile([P, CLASSES], F32)
+            nc.gpsimd.tensor_tensor(
+                out=g_rz[:], in0=tiles["g", i][:], in1=tiles["rz", i][:], op=ALU.mult
+            )
+            tiles["g_rz", i] = g_rz
 
         def gradient(i):
             e = tiles["e", i]
@@ -190,27 +193,24 @@ def tile_lsc_t_v_kernel(tc, x, weights, sims, w_rnorm, grad_out, out):
             )
             tiles["codes", i], tiles["scales", i] = d_codes, d_scales
 
-        def mx_pair(i, half, first_u):
-            if not valid(i):
-                return
-            if first_u == 0:
-                tiles["acc", i, half] = psum_1.tile([P, N_MOVING], F32, name="acc%d" % half)
-            cols = slice(half * N_MOVING, (half + 1) * N_MOVING)
-            for u in (first_u, first_u + 1):
-                toks = slice(u * P, (u + 1) * P)
-                nc.tensor.matmul_mx(
-                    out=tiles["acc", i, half][:],
-                    lhsT=tiles["codes", i][:, toks].bitcast(E5M2X4),
-                    lhsT_scale=tiles["scales", i][:, toks],
-                    rhs=w_codes[:, u, cols].bitcast(E4M3X4), rhs_scale=w_scales[:, u, cols],
-                    start=(u == 0), stop=(u == CLASS_TILES - 1),
-                )
+        def mx_matmuls(i):
+            for half in range(FEATURE_HALVES):
+                cols = slice(half * N_MOVING, (half + 1) * N_MOVING)
+                acc = psum_1.tile([P, N_MOVING], F32, name="acc%d" % half)
+                tiles["acc", i, half] = acc
+                for u in range(CLASS_TILES):
+                    toks = slice(u * P, (u + 1) * P)
+                    nc.tensor.matmul_mx(
+                        out=acc[:],
+                        lhsT=tiles["codes", i][:, toks].bitcast(E5M2X4),
+                        lhsT_scale=tiles["scales", i][:, toks],
+                        rhs=w_codes[:, u, cols].bitcast(E4M3X4), rhs_scale=w_scales[:, u, cols],
+                        start=(u == 0), stop=(u == CLASS_TILES - 1),
+                    )
 
         def leave_psum(i, half):
-            if not valid(i):
-                return
             if half == 0:
-                tiles["y", i] = outs.tile([P, FEATURES], F32, name="y", bufs=3)
+                tiles["y", i] = outs.tile([P, FEATURES], F32, name="y")
                 tiles["dots", i] = outs.tile([P, FEATURE_HALVES], F32, name="dots")
             cols = slice(half * N_MOVING, (half + 1) * N_MOVING)
             acc = tiles["acc", i, half]
@@ -218,20 +218,18 @@ def tile_lsc_t_v_kernel(tc, x, weights, sims, w_rnorm, grad_out, out):
                 out=tiles["y", i][:, cols], in_=acc[:], func=ACT.Copy,
                 scale=tiles["inv_nx", i][:, 0:1],
             )
-            products = outs.tile([P, N_MOVING], F32)
+            products = outs.tile([P, N_MOVING], F32, bufs=1)
             nc.vector.scalar_tensor_tensor(
                 out=products[:], in0=acc[:], scalar=1.0, in1=tiles["x", i][:, cols],
                 op0=ALU.mult, op1=ALU.mult, accum_out=tiles["dots", i][:, half : half + 1],
             )
 
         def project_and_store(i):
-            if not valid(i):
-                return
             y, dots = tiles["y", i], tiles["dots", i]
             coef = outs.tile([P, 1], F32)
             nc.vector.tensor_scalar(
                 out=coef[:], in0=dots[:, 0:1], scalar1=dots[:, 1:2],
-                scalar2=tiles["inv_nx3", i][:, 0:1], op0=ALU.add, op1=ALU.mult,
+                scalar2=tiles["inv_nx", i][:, 1:2], op0=ALU.add, op1=ALU.mult,
             )
             neg_coef = outs.tile([P, 1], F32)
             nc.vector.tensor_scalar(
@@ -251,36 +249,32 @@ def tile_lsc_t_v_kernel(tc, x, weights, sims, w_rnorm, grad_out, out):
         load_inputs(1)
         shift_by_max(0)
         for step in range(STEPS):
-            mx_tile = step - MX_LAG
             if valid(step + 2):
                 load_inputs(step + 2)
-            if step + 1 < CLASS_TILES:
-                load_weights(step + 1)
+            if valid(step - 1):
+                per_class(step - 1)
             if valid(step):
                 transpose_shifted(step)
-            mx_pair(mx_tile, 0, 0)
-            if valid(step):
                 exponentials(step)
             if valid(step + 1):
                 shift_by_max(step + 1)
+            if valid(step - 1):
+                scale_grad_out(step - 1)
             if valid(step):
                 open_proxy_sums(step)
-                proxy_sums(step, 0)
-                proxy_sums(step, 1)
-            mx_pair(mx_tile, 0, 2)
-            if valid(step):
-                proxy_sums(step, 2)
-                proxy_sums(step, 3)
-            mx_pair(mx_tile, 1, 0)
-            leave_psum(mx_tile, 0)
-            if valid(step - 1):
-                gradient(step - 1)
-            mx_pair(mx_tile, 1, 2)
+                for u in range(CLASS_TILES):
+                    proxy_sums(step, u)
+            if valid(step - MX_LAG - 1):
+                leave_psum(step - MX_LAG - 1, 0)
+                leave_psum(step - MX_LAG - 1, 1)
+                project_and_store(step - MX_LAG - 1)
+            if valid(step - 2):
+                gradient(step - 2)
+            if valid(step - MX_LAG):
+                mx_matmuls(step - MX_LAG)
             if valid(step):
                 reciprocals(step)
             if step < CLASS_TILES:
                 prepare_wn(step)
-            if valid(step):
-                per_class(step)
-            leave_psum(mx_tile, 1)
-            project_and_store(mx_tile)
+            if step + 1 < CLASS_TILES:
+                load_weights(step + 1)

@@ -271,7 +271,8 @@ def tile_lsc_t_v_kernel(tc, x, weights, sims, w_rnorm, grad_out, out):
             if valid(step - 2):
                 gradient(step - 2)
             if valid(step - MX_LAG):
-                mx_matmuls(step - MX_LAG)
+                with tc.high_priority():
+                    mx_matmuls(step - MX_LAG)
             if valid(step):
                 reciprocals(step)
             if step < CLASS_TILES:

@@ -47,10 +47,6 @@ def tile_lsc_t_v_kernel(tc, x, weights, sims, w_rnorm, grad_out, out):
         w_codes = consts.tile([P, CLASS_TILES, FEATURES], U32, align_bytes=64)
         w_scales = consts.tile([P, CLASS_TILES, FEATURES], U8, align_bytes=64)
 
-        exponents = consts.tile([P, 2], F32)
-        nc.gpsimd.memset(exponents[:, 0:1], -0.5)
-        nc.gpsimd.memset(exponents[:, 1:2], -1.5)
-
         tiles = {}
 
         def valid(i):
@@ -128,11 +124,7 @@ def tile_lsc_t_v_kernel(tc, x, weights, sims, w_rnorm, grad_out, out):
             nc.scalar.activation(
                 out=x_sq[:], in_=tiles["x", i][:], func=ACT.Square, accum_out=nx2[:]
             )
-            inv_nx = held.tile([P, 2], F32)
-            nc.gpsimd.tensor_tensor(
-                out=inv_nx[:], in0=nx2[:].to_broadcast([P, 2]), in1=exponents[:], op=ALU.pow
-            )
-            tiles["inv_nx", i] = inv_nx
+            tiles["nx2", i] = nx2
 
         def open_proxy_sums(i):
             tiles["z", i] = psum_1.tile([P, CLASSES], F32, name="z_u")
@@ -149,9 +141,15 @@ def tile_lsc_t_v_kernel(tc, x, weights, sims, w_rnorm, grad_out, out):
         def reciprocals(i):
             ln_z = perclass.tile([P, CLASSES], F32, bufs=1)
             nc.scalar.activation(out=ln_z[:], in_=tiles["z", i][:], func=ACT.Ln)
+            ln_nx2 = held.tile([P, 1], F32)
+            nc.scalar.activation(out=ln_nx2[:], in_=tiles["nx2", i][:], func=ACT.Ln)
             rz = perclass.tile([P, CLASSES], F32)
             nc.scalar.activation(out=rz[:], in_=ln_z[:], func=ACT.Exp, scale=-1.0)
-            tiles["rz", i] = rz
+            inv_nx = held.tile([P, 1], F32)
+            nc.scalar.activation(out=inv_nx[:], in_=ln_nx2[:], func=ACT.Exp, scale=-0.5)
+            inv_nx3 = held.tile([P, 1], F32)
+            nc.scalar.activation(out=inv_nx3[:], in_=ln_nx2[:], func=ACT.Exp, scale=-1.5)
+            tiles["rz", i], tiles["inv_nx", i], tiles["inv_nx3", i] = rz, inv_nx, inv_nx3
 
         def per_class(i):
             q = perclass.tile([P, CLASSES], F32)
@@ -229,7 +227,7 @@ def tile_lsc_t_v_kernel(tc, x, weights, sims, w_rnorm, grad_out, out):
             coef = outs.tile([P, 1], F32)
             nc.vector.tensor_scalar(
                 out=coef[:], in0=dots[:, 0:1], scalar1=dots[:, 1:2],
-                scalar2=tiles["inv_nx", i][:, 1:2], op0=ALU.add, op1=ALU.mult,
+                scalar2=tiles["inv_nx3", i][:, 0:1], op0=ALU.add, op1=ALU.mult,
             )
             neg_coef = outs.tile([P, 1], F32)
             nc.vector.tensor_scalar(
@@ -271,8 +269,7 @@ def tile_lsc_t_v_kernel(tc, x, weights, sims, w_rnorm, grad_out, out):
             if valid(step - 2):
                 gradient(step - 2)
             if valid(step - MX_LAG):
-                with tc.high_priority():
-                    mx_matmuls(step - MX_LAG)
+                mx_matmuls(step - MX_LAG)
             if valid(step):
                 reciprocals(step)
             if step < CLASS_TILES:

@@ -47,6 +47,10 @@ def tile_lsc_t_v_kernel(tc, x, weights, sims, w_rnorm, grad_out, out):
         w_codes = consts.tile([P, CLASS_TILES, FEATURES], U32, align_bytes=64)
         w_scales = consts.tile([P, CLASS_TILES, FEATURES], U8, align_bytes=64)
 
+        exponents = consts.tile([P, 2], F32)
+        nc.gpsimd.memset(exponents[:, 0:1], -0.5)
+        nc.gpsimd.memset(exponents[:, 1:2], -1.5)
+
         tiles = {}
 
         def valid(i):
@@ -95,8 +99,9 @@ def tile_lsc_t_v_kernel(tc, x, weights, sims, w_rnorm, grad_out, out):
             )
             planes = big.tile([P, PROXIES, CLASSES], F32, bufs=4)
             nc.gpsimd.tensor_tensor(
-                out=planes[:], in0=tiles["s", i][:].rearrange("b (c p) -> b p c", p=PROXIES),
-                in1=neg_m[:].unsqueeze(1).to_broadcast([P, PROXIES, CLASSES]), op=ALU.add,
+                out=planes[:].rearrange("b p c -> b c p"),
+                in0=tiles["s", i][:].rearrange("b (c p) -> b c p", p=PROXIES),
+                in1=neg_m[:].unsqueeze(2).to_broadcast([P, CLASSES, PROXIES]), op=ALU.add,
             )
             tiles["planes", i] = planes
 
@@ -124,7 +129,11 @@ def tile_lsc_t_v_kernel(tc, x, weights, sims, w_rnorm, grad_out, out):
             nc.scalar.activation(
                 out=x_sq[:], in_=tiles["x", i][:], func=ACT.Square, accum_out=nx2[:]
             )
-            tiles["nx2", i] = nx2
+            inv_nx = held.tile([P, 2], F32)
+            nc.gpsimd.tensor_tensor(
+                out=inv_nx[:], in0=nx2[:].to_broadcast([P, 2]), in1=exponents[:], op=ALU.pow
+            )
+            tiles["inv_nx", i] = inv_nx
 
         def open_proxy_sums(i):
             tiles["z", i] = psum_1.tile([P, CLASSES], F32, name="z_u")
@@ -141,15 +150,9 @@ def tile_lsc_t_v_kernel(tc, x, weights, sims, w_rnorm, grad_out, out):
         def reciprocals(i):
             ln_z = perclass.tile([P, CLASSES], F32, bufs=1)
             nc.scalar.activation(out=ln_z[:], in_=tiles["z", i][:], func=ACT.Ln)
-            ln_nx2 = held.tile([P, 1], F32)
-            nc.scalar.activation(out=ln_nx2[:], in_=tiles["nx2", i][:], func=ACT.Ln)
             rz = perclass.tile([P, CLASSES], F32)
             nc.scalar.activation(out=rz[:], in_=ln_z[:], func=ACT.Exp, scale=-1.0)
-            inv_nx = held.tile([P, 1], F32)
-            nc.scalar.activation(out=inv_nx[:], in_=ln_nx2[:], func=ACT.Exp, scale=-0.5)
-            inv_nx3 = held.tile([P, 1], F32)
-            nc.scalar.activation(out=inv_nx3[:], in_=ln_nx2[:], func=ACT.Exp, scale=-1.5)
-            tiles["rz", i], tiles["inv_nx", i], tiles["inv_nx3", i] = rz, inv_nx, inv_nx3
+            tiles["rz", i] = rz
 
         def per_class(i):
             q = perclass.tile([P, CLASSES], F32)
@@ -227,7 +230,7 @@ def tile_lsc_t_v_kernel(tc, x, weights, sims, w_rnorm, grad_out, out):
             coef = outs.tile([P, 1], F32)
             nc.vector.tensor_scalar(
                 out=coef[:], in0=dots[:, 0:1], scalar1=dots[:, 1:2],
-                scalar2=tiles["inv_nx3", i][:, 0:1], op0=ALU.add, op1=ALU.mult,
+                scalar2=tiles["inv_nx", i][:, 1:2], op0=ALU.add, op1=ALU.mult,
             )
             neg_coef = outs.tile([P, 1], F32)
             nc.vector.tensor_scalar(

@@ -97,19 +97,18 @@ def tile_lsc_t_v_kernel(tc, x, weights, sims, w_rnorm, grad_out, out):
                 out=neg_m[:], in_=tiles["s", i][:].rearrange("b (c p) -> b c p", p=PROXIES),
                 axis=AXIS.X, op=ALU.max, negate=True,
             )
-            planes = big.tile([P, PROXIES, CLASSES], F32, bufs=4)
+            shifted = big.tile([P, CLASSES, PROXIES], F32, bufs=4)
             nc.gpsimd.tensor_tensor(
-                out=planes[:].rearrange("b p c -> b c p"),
-                in0=tiles["s", i][:].rearrange("b (c p) -> b c p", p=PROXIES),
+                out=shifted[:], in0=tiles["s", i][:].rearrange("b (c p) -> b c p", p=PROXIES),
                 in1=neg_m[:].unsqueeze(2).to_broadcast([P, CLASSES, PROXIES]), op=ALU.add,
             )
-            tiles["planes", i] = planes
+            tiles["shifted", i] = shifted
 
         def transpose_planes(i, u):
             bank = psum_t.tile([P, PROXIES, P], F32)
             for p in range(PROXIES):
                 nc.tensor.transpose(
-                    bank[:, p, :], tiles["planes", i][:, p, u * P : (u + 1) * P], ident[:]
+                    bank[:, p, :], tiles["shifted", i][:, u * P : (u + 1) * P, p], ident[:]
                 )
             return bank
 
@@ -157,10 +156,10 @@ def tile_lsc_t_v_kernel(tc, x, weights, sims, w_rnorm, grad_out, out):
         def per_class(i):
             q = perclass.tile([P, CLASSES], F32)
             nc.vector.tensor_tensor(out=q[:], in0=tiles["n", i][:], in1=tiles["rz", i][:], op=ALU.mult)
-            planes = tiles["planes", i]
+            shifted = tiles["shifted", i]
             nc.gpsimd.tensor_tensor(
-                out=planes[:], in0=planes[:],
-                in1=q[:].unsqueeze(1).to_broadcast([P, PROXIES, CLASSES]), op=ALU.subtract,
+                out=shifted[:], in0=shifted[:],
+                in1=q[:].unsqueeze(2).to_broadcast([P, CLASSES, PROXIES]), op=ALU.subtract,
             )
 
         def scale_grad_out(i):

@@ -98,10 +98,13 @@ def tile_lsc_t_v_kernel(tc, x, weights, sims, w_rnorm, grad_out, out):
                 axis=AXIS.X, op=ALU.max, negate=True,
             )
             shifted = big.tile([P, CLASSES, PROXIES], F32, bufs=4)
-            nc.gpsimd.tensor_tensor(
-                out=shifted[:], in0=tiles["s", i][:].rearrange("b (c p) -> b c p", p=PROXIES),
-                in1=neg_m[:].unsqueeze(2).to_broadcast([P, CLASSES, PROXIES]), op=ALU.add,
-            )
+            by_class = tiles["s", i][:].rearrange("b (c p) -> b c p", p=PROXIES)
+            for u in range(CLASS_TILES):
+                cols = slice(u * P, (u + 1) * P)
+                nc.gpsimd.tensor_tensor(
+                    out=shifted[:, cols, :], in0=by_class[:, cols, :],
+                    in1=neg_m[:, cols].unsqueeze(2).to_broadcast([P, P, PROXIES]), op=ALU.add,
+                )
             tiles["shifted", i] = shifted
 
         def transpose_planes(i, u):
@@ -157,10 +160,12 @@ def tile_lsc_t_v_kernel(tc, x, weights, sims, w_rnorm, grad_out, out):
             q = perclass.tile([P, CLASSES], F32)
             nc.vector.tensor_tensor(out=q[:], in0=tiles["n", i][:], in1=tiles["rz", i][:], op=ALU.mult)
             shifted = tiles["shifted", i]
-            nc.gpsimd.tensor_tensor(
-                out=shifted[:], in0=shifted[:],
-                in1=q[:].unsqueeze(2).to_broadcast([P, CLASSES, PROXIES]), op=ALU.subtract,
-            )
+            for u in range(CLASS_TILES):
+                cols = slice(u * P, (u + 1) * P)
+                nc.gpsimd.tensor_tensor(
+                    out=shifted[:, cols, :], in0=shifted[:, cols, :],
+                    in1=q[:, cols].unsqueeze(2).to_broadcast([P, P, PROXIES]), op=ALU.subtract,
+                )
 
         def scale_grad_out(i):
             g_rz = perclass.tile([P, CLASSES], F32)

@@ -22,11 +22,16 @@ TOKEN_TILES = TOKENS // P
 CLASS_TILES = CLASSES // P
 N_MOVING = 512
 FEATURE_HALVES = FEATURES // N_MOVING
-MX_LAG = 4
-STEPS = TOKEN_TILES + MX_LAG + 1
 
 FLOPS = 2 * TOKENS * CLASSES * PROXIES * FEATURES
 
+
+MAX_PIECES = 2
+AS_PIECES = 4
+AS_BUFS = 1
+CODE_BUFS = 5
+MX_LAG = 3
+SCALE_ON_SCALAR = (0,)
 
 def tile_lsc_t_v_kernel(tc, x, weights, sims, w_rnorm, grad_out, out):
     nc = tc.nc
@@ -35,11 +40,11 @@ def tile_lsc_t_v_kernel(tc, x, weights, sims, w_rnorm, grad_out, out):
         wprep = ctx.enter_context(tc.tile_pool(name="wprep", bufs=1))
         loads = ctx.enter_context(tc.tile_pool(name="loads", bufs=3))
         big = ctx.enter_context(tc.tile_pool(name="big", bufs=2))
-        perclass = ctx.enter_context(tc.tile_pool(name="perclass", bufs=2))
-        held = ctx.enter_context(tc.tile_pool(name="held", bufs=MX_LAG + 3))
+        small = ctx.enter_context(tc.tile_pool(name="small", bufs=2))
         outs = ctx.enter_context(tc.tile_pool(name="outs", bufs=2))
-        psum_t = ctx.enter_context(tc.psum_pool(name="psum_t", bufs=3))
+        psum_w = ctx.enter_context(tc.psum_pool(name="psum_w", bufs=4))
         psum_1 = ctx.enter_context(tc.psum_pool(name="psum_1", bufs=1))
+        ctx.enter_context(tc.manual_schedule())
 
         ident = consts.tile([P, P], F32)
         make_identity(nc, ident[:])
@@ -49,237 +54,317 @@ def tile_lsc_t_v_kernel(tc, x, weights, sims, w_rnorm, grad_out, out):
 
         exponents = consts.tile([P, 2], F32)
         nc.gpsimd.memset(exponents[:, 0:1], -0.5)
-        nc.gpsimd.memset(exponents[:, 1:2], -1.5)
+        nc.gpsimd.memset(exponents[:, 1:2], -1.0)
 
         tiles = {}
 
-        def valid(i):
-            return 0 <= i < TOKEN_TILES
+        def block(u):
+            return slice(u * P, (u + 1) * P)
 
-        def load_inputs(i):
+        def half_cols(half):
+            return slice(half * N_MOVING, (half + 1) * N_MOVING)
+
+        def load_sims(i):
             rows = slice(i * P, (i + 1) * P)
             s_sb = loads.tile([P, CLASSES * PROXIES], F32)
             nc.sync.dma_start(out=s_sb[:], in_=sims[rows, :])
-            x_sb = held.tile([P, FEATURES], BF16, bufs=MX_LAG + 5)
-            nc.sync.dma_start(out=x_sb[:], in_=x[rows, :])
-            g_sb = loads.tile([P, CLASSES], BF16, bufs=4)
+            g_sb = loads.tile([P, CLASSES], BF16, bufs=5)
             nc.sync.dma_start(out=g_sb[:], in_=grad_out[rows, :])
-            tiles["s", i], tiles["x", i], tiles["g", i] = s_sb, x_sb, g_sb
+            tiles["s", i], tiles["g", i] = s_sb, g_sb
+
+        def load_x(i):
+            x_sb = loads.tile([P, FEATURES], BF16, bufs=6)
+            nc.sync.dma_start(out=x_sb[:], in_=x[i * P : (i + 1) * P, :])
+            tiles["x", i] = x_sb
 
         def load_weights(u):
-            raw = wprep.tile([P, PROXIES, FEATURES], BF16)
+            raw = wprep.tile([P, PROXIES, FEATURES], BF16, bufs=2)
             nc.sync.dma_start(
                 out=raw[:],
                 in_=weights[u * P : (u + 1) * P, :].rearrange("c (p d) -> c p d", p=PROXIES),
             )
             tiles["raw", u] = raw
 
-        def prepare_wn(u):
+        def scale_wn(u):
             scaled = wprep.tile([P, PROXIES, FEATURES], BF16)
             for p in range(PROXIES):
-                nc.scalar.activation(
-                    out=scaled[:, p, :], in_=tiles["raw", u][:, p, :], func=ACT.Copy,
-                    scale=rnorm[:, u, p : p + 1],
+                nc.vector.tensor_scalar(
+                    out=scaled[:, p, :], in0=tiles["raw", u][:, p, :],
+                    scalar1=rnorm[:, u, p : p + 1], scalar2=None, op0=ALU.mult,
                 )
-            grouped = wprep.tile([P, FEATURES, PROXIES], BF16, align_bytes=64)
+            tiles["scaled", u] = scaled
+            tiles["grouped", u] = wprep.tile([P, FEATURES, PROXIES], BF16, name="grouped", align_bytes=64)
+
+        def group_wn(u, half):
             nc.vector.tensor_copy(
-                out=grouped[:].rearrange("c (n i) p -> c n p i", i=4),
-                in_=scaled[:].rearrange("c p (n i) -> c n p i", i=4),
+                out=tiles["grouped", u][:, half_cols(half), :].rearrange("c (n i) p -> c n p i", i=4),
+                in_=tiles["scaled", u][:, :, half_cols(half)].rearrange("c p (n i) -> c n p i", i=4),
             )
+
+        def quantise_wn(u):
             nc.vector.quantize_mx(
                 out=w_codes[:, u, :].bitcast(E4M3X4), scales=w_scales[:, u, :],
-                in_=grouped[:].rearrange("c d p -> c (d p)"),
+                in_=tiles["grouped", u][:].rearrange("c d p -> c (d p)"),
             )
 
-        def shift_by_max(i):
-            neg_m = perclass.tile([P, CLASSES], F32, bufs=1)
+        def split(i, u):
+            if u == 0:
+                tiles["planes", i] = big.tile([P, PROXIES, CLASSES], F32, name="planes", bufs=3)
+            nc.scalar.copy(
+                out=tiles["planes", i][:, :, block(u)].rearrange("b p c -> b c p"),
+                in_=tiles["s", i][:, u * P * PROXIES : (u + 1) * P * PROXIES].rearrange(
+                    "b (c p) -> b c p", p=PROXIES
+                ),
+            )
+
+        def maximum(i, h):
+            if h == 0:
+                tiles["neg_m", i] = small.tile([P, CLASSES], F32, name="neg_m", bufs=3)
+            n = CLASSES // MAX_PIECES
             nc.vector.tensor_reduce(
-                out=neg_m[:], in_=tiles["s", i][:].rearrange("b (c p) -> b c p", p=PROXIES),
+                out=tiles["neg_m", i][:, h * n : (h + 1) * n],
+                in_=tiles["s", i][:, h * n * PROXIES : (h + 1) * n * PROXIES].rearrange(
+                    "b (c p) -> b c p", p=PROXIES
+                ),
                 axis=AXIS.X, op=ALU.max, negate=True,
             )
-            shifted = big.tile([P, CLASSES, PROXIES], F32, bufs=4)
-            by_class = tiles["s", i][:].rearrange("b (c p) -> b c p", p=PROXIES)
-            for u in range(CLASS_TILES):
-                cols = slice(u * P, (u + 1) * P)
-                nc.gpsimd.tensor_tensor(
-                    out=shifted[:, cols, :], in0=by_class[:, cols, :],
-                    in1=neg_m[:, cols].unsqueeze(2).to_broadcast([P, P, PROXIES]), op=ALU.add,
-                )
-            tiles["shifted", i] = shifted
 
-        def transpose_planes(i, u):
-            bank = psum_t.tile([P, PROXIES, P], F32)
+        def transposed_sum(full, per_class, u):
+            bank = psum_w.tile([P, PROXIES, P], F32)
             for p in range(PROXIES):
-                nc.tensor.transpose(
-                    bank[:, p, :], tiles["shifted", i][:, u * P : (u + 1) * P, p], ident[:]
+                nc.tensor.matmul(
+                    out=bank[:, p, :], lhsT=full[:, p, block(u)], rhs=ident[:],
+                    is_transpose=True, start=True, stop=False,
+                )
+                nc.tensor.matmul(
+                    out=bank[:, p, :], lhsT=per_class[:, block(u)], rhs=ident[:],
+                    is_transpose=True, start=False, stop=True,
                 )
             return bank
 
-        def transpose_shifted(i):
-            tiles["d_t", i] = [transpose_planes(i, u) for u in range(CLASS_TILES)]
+        def shifted(i, u):
+            tiles["d_t", i, u] = transposed_sum(tiles["planes", i], tiles["neg_m", i], u)
 
-        def exponentials(i):
-            e = big.tile([P, CLASS_TILES, PROXIES, P], F32, bufs=3)
-            ed = big.tile([P, CLASS_TILES, PROXIES, P], F32, bufs=1)
-            tiles["e", i], tiles["ed", i] = e, ed
-            for u in range(CLASS_TILES):
-                d_t = tiles["d_t", i][u]
-                nc.scalar.activation(out=e[:, u], in_=d_t[:], func=ACT.Exp)
-                nc.vector.tensor_tensor(out=ed[:, u], in0=d_t[:], in1=e[:, u], op=ALU.mult)
-            nx2 = held.tile([P, 1], F32)
+        def exponential(i, u):
+            if u == 0:
+                tiles["e", i] = big.tile([P, CLASS_TILES, PROXIES, P], F32, name="e", bufs=3)
+            nc.scalar.activation(out=tiles["e", i][:, u], in_=tiles["d_t", i, u][:], func=ACT.Exp)
+
+        def weighted(i, u):
+            if u == 0:
+                tiles["f", i] = big.tile([P, CLASS_TILES, PROXIES, P], F32, name="f", bufs=1)
+            nc.vector.scalar_tensor_tensor(
+                out=tiles["f", i][:, u], in0=tiles["d_t", i, u][:], scalar=-1.0,
+                in1=tiles["e", i][:, u], op0=ALU.add, op1=ALU.mult,
+            )
+
+        def proxy_sums(i, u):
+            if u == 0:
+                tiles["z", i] = psum_1.tile([P, CLASSES], F32, name="z_sum")
+                tiles["fs", i] = psum_1.tile([P, CLASSES], F32, name="f_sum")
+            for src, dst in ((tiles["e", i], tiles["z", i]), (tiles["f", i], tiles["fs", i])):
+                for p in range(PROXIES):
+                    nc.tensor.matmul(
+                        out=dst[:, block(u)], lhsT=src[:, u, p, :], rhs=ident[:],
+                        is_transpose=True, start=(p == 0), stop=(p == PROXIES - 1),
+                    )
+
+        def log_z(i):
+            ln_z = small.tile([P, CLASSES], F32, bufs=1)
+            nc.scalar.activation(out=ln_z[:], in_=tiles["z", i][:], func=ACT.Ln)
+            tiles["ln_z", i] = ln_z
+
+        def recip_z(i):
+            rz = small.tile([P, CLASSES], F32)
+            nc.scalar.activation(out=rz[:], in_=tiles["ln_z", i][:], func=ACT.Exp, scale=-1.0)
+            tiles["rz", i] = rz
+
+        def one_minus_q(i):
+            one_q = small.tile([P, CLASSES], F32, bufs=1)
+            nc.vector.scalar_tensor_tensor(
+                out=one_q[:], in0=tiles["fs", i][:], scalar=-1.0, in1=tiles["rz", i][:],
+                op0=ALU.mult, op1=ALU.mult,
+            )
+            tiles["one_q", i] = one_q
+
+        def factor_a(i):
+            a = small.tile([P, CLASSES], F32)
+            nc.gpsimd.tensor_tensor(out=a[:], in0=tiles["g", i][:], in1=tiles["rz", i][:], op=ALU.mult)
+            tiles["a", i] = a
+
+        def one_minus_pooled(i):
+            one_pooled = small.tile([P, CLASSES], F32, bufs=1)
+            nc.gpsimd.tensor_tensor(
+                out=one_pooled[:], in0=tiles["neg_m", i][:], in1=tiles["one_q", i][:], op=ALU.add
+            )
+            tiles["one_pooled", i] = one_pooled
+
+        def constant_term(i):
+            a_const = small.tile([P, CLASSES], F32)
+            nc.vector.tensor_tensor(
+                out=a_const[:], in0=tiles["a", i][:], in1=tiles["one_pooled", i][:], op=ALU.mult
+            )
+            tiles["a_const", i] = a_const
+
+        def scaled_sims(i, j):
+            if j == 0:
+                tiles["a_sims", i] = big.tile([P, PROXIES, CLASSES], F32, name="a_sims", bufs=AS_BUFS)
+            n = CLASSES // AS_PIECES
+            cols = slice(j * n, (j + 1) * n)
+            nc.gpsimd.tensor_tensor(
+                out=tiles["a_sims", i][:, :, cols], in0=tiles["planes", i][:, :, cols],
+                in1=tiles["a", i][:, cols].unsqueeze(1).to_broadcast([P, PROXIES, n]), op=ALU.mult,
+            )
+
+        def bracket(i, u):
+            tiles["h_t", i, u] = transposed_sum(tiles["a_sims", i], tiles["a_const", i], u)
+
+        def gradient(i, u):
+            if u == 0:
+                tiles["dsims", i] = big.tile(
+                    [P, CLASS_TILES, P, PROXIES], BF16, name="dsims", bufs=1, align_bytes=64
+                )
+            nc.vector.tensor_tensor(
+                out=tiles["dsims", i][:, u], in0=tiles["h_t", i, u][:].rearrange("c p b -> c b p"),
+                in1=tiles["e", i][:, u].rearrange("c p b -> c b p"), op=ALU.mult,
+            )
+
+        def quantise(i):
+            d_codes = small.tile([P, CLASS_TILES * P], U32, bufs=CODE_BUFS, align_bytes=64)
+            d_scales = small.tile([P, CLASS_TILES * P], U8, bufs=CODE_BUFS, align_bytes=64)
+            nc.vector.quantize_mx(
+                out=d_codes[:].bitcast(E5M2X4), scales=d_scales[:],
+                in_=tiles["dsims", i][:].rearrange("c u b p -> c (u b p)"),
+            )
+            tiles["codes", i], tiles["scales", i] = d_codes, d_scales
+
+        def square_x(i):
+            nx2 = outs.tile([P, 1], F32, bufs=4)
             x_sq = outs.tile([P, FEATURES], BF16, bufs=1)
             nc.scalar.activation(
                 out=x_sq[:], in_=tiles["x", i][:], func=ACT.Square, accum_out=nx2[:]
             )
-            inv_nx = held.tile([P, 2], F32)
+            tiles["nx2", i] = nx2
+
+        def norms(i):
+            inv_nx = outs.tile([P, 2], F32, bufs=4)
             nc.gpsimd.tensor_tensor(
-                out=inv_nx[:], in0=nx2[:].to_broadcast([P, 2]), in1=exponents[:], op=ALU.pow
+                out=inv_nx[:], in0=tiles["nx2", i][:].to_broadcast([P, 2]), in1=exponents[:],
+                op=ALU.pow,
             )
             tiles["inv_nx", i] = inv_nx
 
-        def open_proxy_sums(i):
-            tiles["z", i] = psum_1.tile([P, CLASSES], F32, name="z_u")
-            tiles["n", i] = psum_1.tile([P, CLASSES], F32, name="n_u")
-
-        def proxy_sums(i, u):
-            for src, dst in ((tiles["e", i], tiles["z", i]), (tiles["ed", i], tiles["n", i])):
-                for p in range(PROXIES):
-                    nc.tensor.matmul(
-                        out=dst[:, u * P : (u + 1) * P], lhsT=src[:, u, p, :], rhs=ident[:],
-                        is_transpose=True, start=(p == 0), stop=(p == PROXIES - 1),
-                    )
-
-        def reciprocals(i):
-            ln_z = perclass.tile([P, CLASSES], F32, bufs=1)
-            nc.scalar.activation(out=ln_z[:], in_=tiles["z", i][:], func=ACT.Ln)
-            rz = perclass.tile([P, CLASSES], F32)
-            nc.scalar.activation(out=rz[:], in_=ln_z[:], func=ACT.Exp, scale=-1.0)
-            tiles["rz", i] = rz
-
-        def per_class(i):
-            q = perclass.tile([P, CLASSES], F32)
-            nc.vector.tensor_tensor(out=q[:], in0=tiles["n", i][:], in1=tiles["rz", i][:], op=ALU.mult)
-            shifted = tiles["shifted", i]
+        def mx_matmuls(i, half):
+            acc = psum_1.tile([P, N_MOVING], F32, name="acc%d" % half)
+            tiles["acc", i, half] = acc
             for u in range(CLASS_TILES):
-                cols = slice(u * P, (u + 1) * P)
-                nc.gpsimd.tensor_tensor(
-                    out=shifted[:, cols, :], in0=shifted[:, cols, :],
-                    in1=q[:, cols].unsqueeze(2).to_broadcast([P, P, PROXIES]), op=ALU.subtract,
+                nc.tensor.matmul_mx(
+                    out=acc[:],
+                    lhsT=tiles["codes", i][:, block(u)].bitcast(E5M2X4),
+                    lhsT_scale=tiles["scales", i][:, block(u)],
+                    rhs=w_codes[:, u, half_cols(half)].bitcast(E4M3X4),
+                    rhs_scale=w_scales[:, u, half_cols(half)],
+                    start=(u == 0), stop=(u == CLASS_TILES - 1),
                 )
 
-        def scale_grad_out(i):
-            g_rz = perclass.tile([P, CLASSES], F32)
-            nc.gpsimd.tensor_tensor(
-                out=g_rz[:], in0=tiles["g", i][:], in1=tiles["rz", i][:], op=ALU.mult
-            )
-            tiles["g_rz", i] = g_rz
-
-        def gradient(i):
-            e = tiles["e", i]
-            r = big.tile([P, CLASS_TILES, PROXIES, P], F32, bufs=1)
-            for u in range(CLASS_TILES):
-                h_t = transpose_planes(i, u)
-                nc.vector.scalar_tensor_tensor(
-                    out=r[:, u], in0=h_t[:], scalar=1.0, in1=e[:, u], op0=ALU.add, op1=ALU.mult
-                )
-            a_t = psum_1.tile([P, CLASS_TILES, P], F32)
-            for u in range(CLASS_TILES):
-                nc.tensor.transpose(a_t[:, u, :], tiles["g_rz", i][:, u * P : (u + 1) * P], ident[:])
-            dsims = big.tile([P, CLASS_TILES, P, PROXIES], BF16, align_bytes=64)
-            nc.vector.tensor_tensor(
-                out=dsims[:], in0=r[:].rearrange("c u p b -> c u b p"),
-                in1=a_t[:].unsqueeze(3).to_broadcast([P, CLASS_TILES, P, PROXIES]), op=ALU.mult,
-            )
-            d_codes = held.tile([P, CLASS_TILES * P], U32, bufs=MX_LAG + 1, align_bytes=64)
-            d_scales = held.tile([P, CLASS_TILES * P], U8, bufs=MX_LAG + 1, align_bytes=64)
-            nc.vector.quantize_mx(
-                out=d_codes[:].bitcast(E5M2X4), scales=d_scales[:],
-                in_=dsims[:].rearrange("c u b p -> c (u b p)"),
-            )
-            tiles["codes", i], tiles["scales", i] = d_codes, d_scales
-
-        def mx_matmuls(i):
-            for half in range(FEATURE_HALVES):
-                cols = slice(half * N_MOVING, (half + 1) * N_MOVING)
-                acc = psum_1.tile([P, N_MOVING], F32, name="acc%d" % half)
-                tiles["acc", i, half] = acc
-                for u in range(CLASS_TILES):
-                    toks = slice(u * P, (u + 1) * P)
-                    nc.tensor.matmul_mx(
-                        out=acc[:],
-                        lhsT=tiles["codes", i][:, toks].bitcast(E5M2X4),
-                        lhsT_scale=tiles["scales", i][:, toks],
-                        rhs=w_codes[:, u, cols].bitcast(E4M3X4), rhs_scale=w_scales[:, u, cols],
-                        start=(u == 0), stop=(u == CLASS_TILES - 1),
-                    )
-
-        def leave_psum(i, half):
+        def dot(i, half):
             if half == 0:
-                tiles["y", i] = outs.tile([P, FEATURES], F32, name="y")
                 tiles["dots", i] = outs.tile([P, FEATURE_HALVES], F32, name="dots")
-            cols = slice(half * N_MOVING, (half + 1) * N_MOVING)
-            acc = tiles["acc", i, half]
-            nc.scalar.activation(
-                out=tiles["y", i][:, cols], in_=acc[:], func=ACT.Copy,
-                scale=tiles["inv_nx", i][:, 0:1],
-            )
             products = outs.tile([P, N_MOVING], F32, bufs=1)
             nc.vector.scalar_tensor_tensor(
-                out=products[:], in0=acc[:], scalar=1.0, in1=tiles["x", i][:, cols],
-                op0=ALU.mult, op1=ALU.mult, accum_out=tiles["dots", i][:, half : half + 1],
+                out=products[:], in0=tiles["acc", i, half][:], scalar=-1.0,
+                in1=tiles["x", i][:, half_cols(half)], op0=ALU.mult, op1=ALU.mult,
+                accum_out=tiles["dots", i][:, half : half + 1],
             )
 
-        def project_and_store(i):
-            y, dots = tiles["y", i], tiles["dots", i]
-            coef = outs.tile([P, 1], F32)
-            nc.vector.tensor_scalar(
-                out=coef[:], in0=dots[:, 0:1], scalar1=dots[:, 1:2],
+        def coefficient(i):
+            neg_c = outs.tile([P, 1], F32)
+            nc.gpsimd.tensor_scalar(
+                out=neg_c[:], in0=tiles["dots", i][:, 0:1], scalar1=tiles["dots", i][:, 1:2],
                 scalar2=tiles["inv_nx", i][:, 1:2], op0=ALU.add, op1=ALU.mult,
             )
-            neg_coef = outs.tile([P, 1], F32)
-            nc.vector.tensor_scalar(
-                out=neg_coef[:], in0=coef[:], scalar1=-1.0, scalar2=None, op0=ALU.mult
-            )
+            tiles["neg_c", i] = neg_c
+
+        def project(i, half):
+            if half == 0:
+                tiles["zed", i] = outs.tile([P, FEATURES], F32, name="zed")
             nc.vector.scalar_tensor_tensor(
-                out=y[:], in0=tiles["x", i][:], scalar=neg_coef[:, 0:1], in1=y[:],
+                out=tiles["zed", i][:, half_cols(half)], in0=tiles["x", i][:, half_cols(half)],
+                scalar=tiles["neg_c", i][:, 0:1], in1=tiles["acc", i, half][:],
                 op0=ALU.mult, op1=ALU.add,
             )
-            nc.sync.dma_start(out=out[i * P : (i + 1) * P, :], in_=y[:])
 
-        load_inputs(0)
+        def divide_by_nx(i, half):
+            if half == 0:
+                tiles["y", i] = outs.tile([P, FEATURES], F32, name="y")
+            if half in SCALE_ON_SCALAR:
+                nc.scalar.activation(
+                    out=tiles["y", i][:, half_cols(half)], in_=tiles["zed", i][:, half_cols(half)],
+                    func=ACT.Copy, scale=tiles["inv_nx", i][:, 0:1],
+                )
+            else:
+                nc.gpsimd.tensor_scalar(
+                    out=tiles["y", i][:, half_cols(half)], in0=tiles["zed", i][:, half_cols(half)],
+                    scalar1=tiles["inv_nx", i][:, 0:1], scalar2=0.0, op0=ALU.mult, op1=ALU.add,
+                )
+
+        def store(i):
+            nc.sync.dma_start(out=out[i * P : (i + 1) * P, :], in_=tiles["y", i][:])
+
+        def do(fn, i, *args):
+            if 0 <= i < TOKEN_TILES:
+                fn(i, *args)
+
+        load_sims(0)
         nc.sync.dma_start(
             out=rnorm[:], in_=w_rnorm.rearrange("(u c p) -> c u p", u=CLASS_TILES, p=PROXIES)
         )
         load_weights(0)
-        load_inputs(1)
-        shift_by_max(0)
-        for step in range(STEPS):
-            if valid(step + 2):
-                load_inputs(step + 2)
-            if valid(step - 1):
-                per_class(step - 1)
-            if valid(step):
-                transpose_shifted(step)
-                exponentials(step)
-            if valid(step + 1):
-                shift_by_max(step + 1)
-            if valid(step - 1):
-                scale_grad_out(step - 1)
-            if valid(step):
-                open_proxy_sums(step)
-                for u in range(CLASS_TILES):
-                    proxy_sums(step, u)
-            if valid(step - MX_LAG - 1):
-                leave_psum(step - MX_LAG - 1, 0)
-                leave_psum(step - MX_LAG - 1, 1)
-                project_and_store(step - MX_LAG - 1)
-            if valid(step - 2):
-                gradient(step - 2)
-            if valid(step - MX_LAG):
-                mx_matmuls(step - MX_LAG)
-            if valid(step):
-                reciprocals(step)
-            if step < CLASS_TILES:
-                prepare_wn(step)
-            if step + 1 < CLASS_TILES:
-                load_weights(step + 1)
+        load_sims(1)
+        load_weights(1)
+        load_sims(2)
+        for t in range(-1, TOKEN_TILES + MX_LAG + 2):
+            late = t - MX_LAG
+            do(project, late - 1, 0)
+            for u in range(CLASS_TILES):
+                do(exponential, t, u)
+                do(weighted, t, u)
+                do(proxy_sums, t, u)
+            do(square_x, late + 1)
+            do(project, late - 1, 1)
+            do(maximum, t + 1, 0)
+            for j in range(AS_PIECES):
+                do(scaled_sims, t - 1, j)
+            for u in range(CLASS_TILES):
+                do(bracket, t - 1, u)
+                do(gradient, t - 1, u)
+            do(quantise, t - 1)
+            for half in range(FEATURE_HALVES):
+                do(divide_by_nx, late - 1, half)
+            do(store, late - 1)
+            do(norms, late + 1)
+            do(log_z, t)
+            do(recip_z, t)
+            do(maximum, t + 1, 1)
+            if 0 <= t + 1 < CLASS_TILES:
+                scale_wn(t + 1)
+                group_wn(t + 1, 0)
+            do(one_minus_q, t)
+            do(factor_a, t)
+            do(one_minus_pooled, t)
+            if 0 <= t + 1 < CLASS_TILES:
+                group_wn(t + 1, 1)
+                quantise_wn(t + 1)
+                if t + 3 < CLASS_TILES:
+                    load_weights(t + 3)
+            for half in range(FEATURE_HALVES):
+                do(mx_matmuls, late, half)
+            for u in range(CLASS_TILES):
+                do(split, t + 1, u)
+                do(shifted, t + 1, u)
+            for half in range(FEATURE_HALVES):
+                do(dot, late, half)
+            do(coefficient, late)
+            do(constant_term, t)
+            do(load_sims, t + 4)
+            do(load_x, late + 3)

@@ -43,7 +43,7 @@ def tile_lsc_t_v_kernel(tc, x, weights, sims, w_rnorm, grad_out, out):
         small = ctx.enter_context(tc.tile_pool(name="small", bufs=2))
         outs = ctx.enter_context(tc.tile_pool(name="outs", bufs=2))
         psum_w = ctx.enter_context(tc.psum_pool(name="psum_w", bufs=4))
-        psum_1 = ctx.enter_context(tc.psum_pool(name="psum_1", bufs=1))
+        psum_1 = ctx.enter_context(tc.psum_pool(name="psum_1", bufs=4))
         ctx.enter_context(tc.manual_schedule())
 
         ident = consts.tile([P, P], F32)
@@ -160,8 +160,8 @@ def tile_lsc_t_v_kernel(tc, x, weights, sims, w_rnorm, grad_out, out):
 
         def proxy_sums(i, u):
             if u == 0:
-                tiles["z", i] = psum_1.tile([P, CLASSES], F32, name="z_sum")
-                tiles["fs", i] = psum_1.tile([P, CLASSES], F32, name="f_sum")
+                tiles["z", i] = psum_1.tile([P, CLASSES], F32, name="sums")
+                tiles["fs", i] = psum_1.tile([P, CLASSES], F32, name="sums")
             for src, dst in ((tiles["e", i], tiles["z", i]), (tiles["f", i], tiles["fs", i])):
                 for p in range(PROXIES):
                     nc.tensor.matmul(
@@ -255,7 +255,7 @@ def tile_lsc_t_v_kernel(tc, x, weights, sims, w_rnorm, grad_out, out):
             tiles["inv_nx", i] = inv_nx
 
         def mx_matmuls(i, half):
-            acc = psum_1.tile([P, N_MOVING], F32, name="acc%d" % half)
+            acc = psum_1.tile([P, N_MOVING], F32, name="sums")
             tiles["acc", i, half] = acc
             for u in range(CLASS_TILES):
                 nc.tensor.matmul_mx(
@@ -315,6 +315,15 @@ def tile_lsc_t_v_kernel(tc, x, weights, sims, w_rnorm, grad_out, out):
             if 0 <= i < TOKEN_TILES:
                 fn(i, *args)
 
+        def matmul_tiles(t):
+            if t < TOKEN_TILES:
+                return [t - MX_LAG]
+            if t == TOKEN_TILES:
+                return list(range(t - MX_LAG, TOKEN_TILES - 1))
+            if t == TOKEN_TILES + 1:
+                return [TOKEN_TILES - 1]
+            return []
+
         load_sims(0)
         nc.sync.dma_start(
             out=rnorm[:], in_=w_rnorm.rearrange("(u c p) -> c u p", u=CLASS_TILES, p=PROXIES)
@@ -323,48 +332,65 @@ def tile_lsc_t_v_kernel(tc, x, weights, sims, w_rnorm, grad_out, out):
         load_sims(1)
         load_weights(1)
         load_sims(2)
-        for t in range(-1, TOKEN_TILES + MX_LAG + 2):
-            late = t - MX_LAG
-            do(project, late - 1, 0)
+        for t in range(-1, TOKEN_TILES + 3):
+            now, before = matmul_tiles(t), matmul_tiles(t - 1)
+            draining = t >= TOKEN_TILES
+            for i in before:
+                do(project, i, 0)
             for u in range(CLASS_TILES):
                 do(exponential, t, u)
                 do(weighted, t, u)
                 do(proxy_sums, t, u)
-            do(square_x, late + 1)
-            do(project, late - 1, 1)
+            do(square_x, t - MX_LAG + 1)
+            for i in before:
+                do(project, i, 1)
+            if draining:
+                for i in now:
+                    for half in range(FEATURE_HALVES):
+                        do(mx_matmuls, i, half)
+                    for half in range(FEATURE_HALVES):
+                        do(dot, i, half)
+            if 0 <= t < CLASS_TILES:
+                group_wn(t, 1)
             do(maximum, t + 1, 0)
+            if 0 <= t < CLASS_TILES:
+                quantise_wn(t)
+                if t + 2 < CLASS_TILES:
+                    load_weights(t + 2)
             for j in range(AS_PIECES):
                 do(scaled_sims, t - 1, j)
             for u in range(CLASS_TILES):
                 do(bracket, t - 1, u)
                 do(gradient, t - 1, u)
-            do(quantise, t - 1)
-            for half in range(FEATURE_HALVES):
-                do(divide_by_nx, late - 1, half)
-            do(store, late - 1)
-            do(norms, late + 1)
+            for i in before:
+                for half in range(FEATURE_HALVES):
+                    do(divide_by_nx, i, half)
+                do(store, i)
+            do(norms, t - MX_LAG + 1)
             do(log_z, t)
             do(recip_z, t)
             do(maximum, t + 1, 1)
+            do(quantise, t - 1)
             if 0 <= t + 1 < CLASS_TILES:
                 scale_wn(t + 1)
-                group_wn(t + 1, 0)
             do(one_minus_q, t)
             do(factor_a, t)
             do(one_minus_pooled, t)
             if 0 <= t + 1 < CLASS_TILES:
-                group_wn(t + 1, 1)
-                quantise_wn(t + 1)
-                if t + 3 < CLASS_TILES:
-                    load_weights(t + 3)
-            for half in range(FEATURE_HALVES):
-                do(mx_matmuls, late, half)
+                group_wn(t + 1, 0)
+            if not draining:
+                for i in now:
+                    for half in range(FEATURE_HALVES):
+                        do(mx_matmuls, i, half)
             for u in range(CLASS_TILES):
                 do(split, t + 1, u)
                 do(shifted, t + 1, u)
-            for half in range(FEATURE_HALVES):
-                do(dot, late, half)
-            do(coefficient, late)
+            if not draining:
+                for i in now:
+                    for half in range(FEATURE_HALVES):
+                        do(dot, i, half)
+            for i in now:
+                do(coefficient, i)
             do(constant_term, t)
             do(load_sims, t + 4)
-            do(load_x, late + 3)
+            do(load_x, t)

@@ -31,7 +31,7 @@ AS_PIECES = 4
 AS_BUFS = 1
 CODE_BUFS = 5
 MX_LAG = 3
-SCALE_ON_SCALAR = (0,)
+SCALE_ON_SCALAR = ()
 
 def tile_lsc_t_v_kernel(tc, x, weights, sims, w_rnorm, grad_out, out):
     nc = tc.nc

@@ -26,12 +26,13 @@ FEATURE_HALVES = FEATURES // N_MOVING
 FLOPS = 2 * TOKENS * CLASSES * PROXIES * FEATURES
 
 
-MAX_PIECES = 2
-AS_PIECES = 4
-AS_BUFS = 1
-CODE_BUFS = 5
+MAX_PIECES = 1
+AS_PIECES = 2
+AS_BUFS = 2
+CODE_BUFS = 4
 MX_LAG = 3
-SCALE_ON_SCALAR = ()
+SCALE_ON_SCALAR = (0,)
+GROUP_ON = ("vector", "vector")
 
 def tile_lsc_t_v_kernel(tc, x, weights, sims, w_rnorm, grad_out, out):
     nc = tc.nc
@@ -68,7 +69,7 @@ def tile_lsc_t_v_kernel(tc, x, weights, sims, w_rnorm, grad_out, out):
             rows = slice(i * P, (i + 1) * P)
             s_sb = loads.tile([P, CLASSES * PROXIES], F32)
             nc.sync.dma_start(out=s_sb[:], in_=sims[rows, :])
-            g_sb = loads.tile([P, CLASSES], BF16, bufs=5)
+            g_sb = loads.tile([P, CLASSES], BF16, bufs=6)
             nc.sync.dma_start(out=g_sb[:], in_=grad_out[rows, :])
             tiles["s", i], tiles["g", i] = s_sb, g_sb
 
@@ -96,10 +97,14 @@ def tile_lsc_t_v_kernel(tc, x, weights, sims, w_rnorm, grad_out, out):
             tiles["grouped", u] = wprep.tile([P, FEATURES, PROXIES], BF16, name="grouped", align_bytes=64)
 
         def group_wn(u, half):
-            nc.vector.tensor_copy(
-                out=tiles["grouped", u][:, half_cols(half), :].rearrange("c (n i) p -> c n p i", i=4),
-                in_=tiles["scaled", u][:, :, half_cols(half)].rearrange("c p (n i) -> c n p i", i=4),
-            )
+            dst = tiles["grouped", u][:, half_cols(half), :].rearrange("c (n i) p -> c n p i", i=4)
+            src = tiles["scaled", u][:, :, half_cols(half)].rearrange("c p (n i) -> c n p i", i=4)
+            if GROUP_ON[half] == "scalar":
+                nc.scalar.copy(out=dst, in_=src)
+            elif GROUP_ON[half] == "gpsimd":
+                nc.gpsimd.tensor_scalar(out=dst, in0=src, scalar1=1.0, scalar2=0.0, op0=ALU.mult, op1=ALU.add)
+            else:
+                nc.vector.tensor_copy(out=dst, in_=src)
 
         def quantise_wn(u):
             nc.vector.quantize_mx(
@@ -119,7 +124,7 @@ def tile_lsc_t_v_kernel(tc, x, weights, sims, w_rnorm, grad_out, out):
 
         def maximum(i, h):
             if h == 0:
-                tiles["neg_m", i] = small.tile([P, CLASSES], F32, name="neg_m", bufs=3)
+                tiles["neg_m", i] = small.tile([P, CLASSES], F32, name="neg_m", bufs=4)
             n = CLASSES // MAX_PIECES
             nc.vector.tensor_reduce(
                 out=tiles["neg_m", i][:, h * n : (h + 1) * n],
@@ -201,7 +206,7 @@ def tile_lsc_t_v_kernel(tc, x, weights, sims, w_rnorm, grad_out, out):
 
         def constant_term(i):
             a_const = small.tile([P, CLASSES], F32)
-            nc.vector.tensor_tensor(
+            nc.gpsimd.tensor_tensor(
                 out=a_const[:], in0=tiles["a", i][:], in1=tiles["one_pooled", i][:], op=ALU.mult
             )
             tiles["a_const", i] = a_const
@@ -319,8 +324,10 @@ def tile_lsc_t_v_kernel(tc, x, weights, sims, w_rnorm, grad_out, out):
             if t < TOKEN_TILES:
                 return [t - MX_LAG]
             if t == TOKEN_TILES:
-                return list(range(t - MX_LAG, TOKEN_TILES - 1))
+                return [t - MX_LAG]
             if t == TOKEN_TILES + 1:
+                return [TOKEN_TILES - 2]
+            if t == TOKEN_TILES + 2:
                 return [TOKEN_TILES - 1]
             return []
 
@@ -332,65 +339,57 @@ def tile_lsc_t_v_kernel(tc, x, weights, sims, w_rnorm, grad_out, out):
         load_sims(1)
         load_weights(1)
         load_sims(2)
-        for t in range(-1, TOKEN_TILES + 3):
+        for t in range(-1, TOKEN_TILES + 4):
             now, before = matmul_tiles(t), matmul_tiles(t - 1)
-            draining = t >= TOKEN_TILES
-            for i in before:
-                do(project, i, 0)
+            preparing = 0 <= t < CLASS_TILES
+            do(one_minus_q, t - 1)
             for u in range(CLASS_TILES):
                 do(exponential, t, u)
                 do(weighted, t, u)
                 do(proxy_sums, t, u)
+            for u in range(CLASS_TILES):
+                do(split, t + 1, u)
             do(square_x, t - MX_LAG + 1)
-            for i in before:
-                do(project, i, 1)
-            if draining:
-                for i in now:
-                    for half in range(FEATURE_HALVES):
-                        do(mx_matmuls, i, half)
-                    for half in range(FEATURE_HALVES):
-                        do(dot, i, half)
-            if 0 <= t < CLASS_TILES:
+            do(factor_a, t - 1)
+            do(one_minus_pooled, t - 1)
+            do(constant_term, t - 1)
+            for j in range(AS_PIECES):
+                do(scaled_sims, t - 1, j)
+            if preparing:
                 group_wn(t, 1)
-            do(maximum, t + 1, 0)
-            if 0 <= t < CLASS_TILES:
+            for i in before:
+                for half in range(FEATURE_HALVES):
+                    do(project, i, half)
+            if preparing:
                 quantise_wn(t)
                 if t + 2 < CLASS_TILES:
                     load_weights(t + 2)
-            for j in range(AS_PIECES):
-                do(scaled_sims, t - 1, j)
+            for i in now:
+                for half in range(FEATURE_HALVES):
+                    do(mx_matmuls, i, half)
+            for h in range(MAX_PIECES):
+                do(maximum, t + 1, h)
+            for i in now:
+                do(dot, i, 0)
             for u in range(CLASS_TILES):
-                do(bracket, t - 1, u)
-                do(gradient, t - 1, u)
+                do(bracket, t - 2, u)
+                do(gradient, t - 2, u)
+            do(log_z, t)
+            do(recip_z, t)
+            for u in range(CLASS_TILES):
+                do(shifted, t + 1, u)
             for i in before:
                 for half in range(FEATURE_HALVES):
                     do(divide_by_nx, i, half)
                 do(store, i)
             do(norms, t - MX_LAG + 1)
-            do(log_z, t)
-            do(recip_z, t)
-            do(maximum, t + 1, 1)
-            do(quantise, t - 1)
-            if 0 <= t + 1 < CLASS_TILES:
-                scale_wn(t + 1)
-            do(one_minus_q, t)
-            do(factor_a, t)
-            do(one_minus_pooled, t)
-            if 0 <= t + 1 < CLASS_TILES:
-                group_wn(t + 1, 0)
-            if not draining:
-                for i in now:
-                    for half in range(FEATURE_HALVES):
-                        do(mx_matmuls, i, half)
-            for u in range(CLASS_TILES):
-                do(split, t + 1, u)
-                do(shifted, t + 1, u)
-            if not draining:
-                for i in now:
-                    for half in range(FEATURE_HALVES):
-                        do(dot, i, half)
+            for i in now:
+                do(dot, i, 1)
+            do(quantise, t - 2)
             for i in now:
                 do(coefficient, i)
-            do(constant_term, t)
+            if 0 <= t + 1 < CLASS_TILES:
+                scale_wn(t + 1)
+                group_wn(t + 1, 0)
             do(load_sims, t + 4)
             do(load_x, t)

@@ -26,13 +26,14 @@ FEATURE_HALVES = FEATURES // N_MOVING
 FLOPS = 2 * TOKENS * CLASSES * PROXIES * FEATURES
 
 
-MAX_PIECES = 1
 AS_PIECES = 2
 AS_BUFS = 2
 CODE_BUFS = 4
 MX_LAG = 3
-SCALE_ON_SCALAR = (0,)
+SCALE_ON_SCALAR = (0, 1)
 GROUP_ON = ("vector", "vector")
+FIRST_PIECES = 4
+WARM_TABLE = True
 
 def tile_lsc_t_v_kernel(tc, x, weights, sims, w_rnorm, grad_out, out):
     nc = tc.nc
@@ -59,6 +60,13 @@ def tile_lsc_t_v_kernel(tc, x, weights, sims, w_rnorm, grad_out, out):
 
         tiles = {}
 
+        if WARM_TABLE:
+            warm = consts.tile([P, 1], F32)
+            nc.scalar.activation(out=warm[:], in_=exponents[:, 0:1], func=ACT.Exp)
+
+        def pieces_of(i):
+            return FIRST_PIECES if i == 0 else 1
+
         def block(u):
             return slice(u * P, (u + 1) * P)
 
@@ -68,7 +76,9 @@ def tile_lsc_t_v_kernel(tc, x, weights, sims, w_rnorm, grad_out, out):
         def load_sims(i):
             rows = slice(i * P, (i + 1) * P)
             s_sb = loads.tile([P, CLASSES * PROXIES], F32)
-            nc.sync.dma_start(out=s_sb[:], in_=sims[rows, :])
+            n = CLASSES * PROXIES // pieces_of(i)
+            for j in range(pieces_of(i)):
+                nc.sync.dma_start(out=s_sb[:, j * n : (j + 1) * n], in_=sims[rows, j * n : (j + 1) * n])
             g_sb = loads.tile([P, CLASSES], BF16, bufs=6)
             nc.sync.dma_start(out=g_sb[:], in_=grad_out[rows, :])
             tiles["s", i], tiles["g", i] = s_sb, g_sb
@@ -112,23 +122,24 @@ def tile_lsc_t_v_kernel(tc, x, weights, sims, w_rnorm, grad_out, out):
                 in_=tiles["grouped", u][:].rearrange("c d p -> c (d p)"),
             )
 
-        def split(i, u):
-            if u == 0:
+        def split(i, j):
+            if j == 0:
                 tiles["planes", i] = big.tile([P, PROXIES, CLASSES], F32, name="planes", bufs=3)
+            n = CLASSES // pieces_of(i)
             nc.scalar.copy(
-                out=tiles["planes", i][:, :, block(u)].rearrange("b p c -> b c p"),
-                in_=tiles["s", i][:, u * P * PROXIES : (u + 1) * P * PROXIES].rearrange(
+                out=tiles["planes", i][:, :, j * n : (j + 1) * n].rearrange("b p c -> b c p"),
+                in_=tiles["s", i][:, j * n * PROXIES : (j + 1) * n * PROXIES].rearrange(
                     "b (c p) -> b c p", p=PROXIES
                 ),
             )
 
-        def maximum(i, h):
-            if h == 0:
+        def maximum(i, j):
+            if j == 0:
                 tiles["neg_m", i] = small.tile([P, CLASSES], F32, name="neg_m", bufs=4)
-            n = CLASSES // MAX_PIECES
+            n = CLASSES // pieces_of(i)
             nc.vector.tensor_reduce(
-                out=tiles["neg_m", i][:, h * n : (h + 1) * n],
-                in_=tiles["s", i][:, h * n * PROXIES : (h + 1) * n * PROXIES].rearrange(
+                out=tiles["neg_m", i][:, j * n : (j + 1) * n],
+                in_=tiles["s", i][:, j * n * PROXIES : (j + 1) * n * PROXIES].rearrange(
                     "b (c p) -> b c p", p=PROXIES
                 ),
                 axis=AXIS.X, op=ALU.max, negate=True,
@@ -347,8 +358,8 @@ def tile_lsc_t_v_kernel(tc, x, weights, sims, w_rnorm, grad_out, out):
                 do(exponential, t, u)
                 do(weighted, t, u)
                 do(proxy_sums, t, u)
-            for u in range(CLASS_TILES):
-                do(split, t + 1, u)
+            for j in range(pieces_of(t + 1)):
+                do(split, t + 1, j)
             do(square_x, t - MX_LAG + 1)
             do(factor_a, t - 1)
             do(one_minus_pooled, t - 1)
@@ -367,8 +378,8 @@ def tile_lsc_t_v_kernel(tc, x, weights, sims, w_rnorm, grad_out, out):
             for i in now:
                 for half in range(FEATURE_HALVES):
                     do(mx_matmuls, i, half)
-            for h in range(MAX_PIECES):
-                do(maximum, t + 1, h)
+            for j in range(pieces_of(t + 1)):
+                do(maximum, t + 1, j)
             for i in now:
                 do(dot, i, 0)
             for u in range(CLASS_TILES):

@@ -28,8 +28,8 @@ FLOPS = 2 * TOKENS * CLASSES * PROXIES * FEATURES
 
 AS_PIECES = 2
 AS_BUFS = 2
-CODE_BUFS = 4
-MX_LAG = 3
+CODE_BUFS = 5
+MX_LAG = 4
 SCALE_ON_SCALAR = (0, 1)
 GROUP_ON = ("vector", "vector")
 FIRST_PIECES = 4
@@ -84,7 +84,7 @@ def tile_lsc_t_v_kernel(tc, x, weights, sims, w_rnorm, grad_out, out):
             tiles["s", i], tiles["g", i] = s_sb, g_sb
 
         def load_x(i):
-            x_sb = loads.tile([P, FEATURES], BF16, bufs=6)
+            x_sb = loads.tile([P, FEATURES], BF16, bufs=7)
             nc.sync.dma_start(out=x_sb[:], in_=x[i * P : (i + 1) * P, :])
             tiles["x", i] = x_sb
 
@@ -135,7 +135,7 @@ def tile_lsc_t_v_kernel(tc, x, weights, sims, w_rnorm, grad_out, out):
 
         def maximum(i, j):
             if j == 0:
-                tiles["neg_m", i] = small.tile([P, CLASSES], F32, name="neg_m", bufs=4)
+                tiles["neg_m", i] = small.tile([P, CLASSES], F32, name="neg_m", bufs=5)
             n = CLASSES // pieces_of(i)
             nc.vector.tensor_reduce(
                 out=tiles["neg_m", i][:, j * n : (j + 1) * n],
@@ -303,7 +303,7 @@ def tile_lsc_t_v_kernel(tc, x, weights, sims, w_rnorm, grad_out, out):
 
         def project(i, half):
             if half == 0:
-                tiles["zed", i] = outs.tile([P, FEATURES], F32, name="zed")
+                tiles["zed", i] = outs.tile([P, FEATURES], F32, name="zed", bufs=1)
             nc.vector.scalar_tensor_tensor(
                 out=tiles["zed", i][:, half_cols(half)], in0=tiles["x", i][:, half_cols(half)],
                 scalar=tiles["neg_c", i][:, 0:1], in1=tiles["acc", i, half][:],
@@ -332,15 +332,7 @@ def tile_lsc_t_v_kernel(tc, x, weights, sims, w_rnorm, grad_out, out):
                 fn(i, *args)
 
         def matmul_tiles(t):
-            if t < TOKEN_TILES:
-                return [t - MX_LAG]
-            if t == TOKEN_TILES:
-                return [t - MX_LAG]
-            if t == TOKEN_TILES + 1:
-                return [TOKEN_TILES - 2]
-            if t == TOKEN_TILES + 2:
-                return [TOKEN_TILES - 1]
-            return []
+            return [t - MX_LAG] if 0 <= t - MX_LAG < TOKEN_TILES else []
 
         load_sims(0)
         nc.sync.dma_start(
@@ -350,9 +342,17 @@ def tile_lsc_t_v_kernel(tc, x, weights, sims, w_rnorm, grad_out, out):
         load_sims(1)
         load_weights(1)
         load_sims(2)
-        for t in range(-1, TOKEN_TILES + 4):
+        for j in range(pieces_of(0)):
+            maximum(0, j)
+        for t in range(-1, TOKEN_TILES + MX_LAG + 1):
             now, before = matmul_tiles(t), matmul_tiles(t - 1)
-            preparing = 0 <= t < CLASS_TILES
+            preparing = 0 <= t + 1 < CLASS_TILES
+            for i in before:
+                for half in range(FEATURE_HALVES):
+                    do(project, i, half)
+            for i in now:
+                for half in range(FEATURE_HALVES):
+                    do(mx_matmuls, i, half)
             do(one_minus_q, t - 1)
             for u in range(CLASS_TILES):
                 do(exponential, t, u)
@@ -364,24 +364,18 @@ def tile_lsc_t_v_kernel(tc, x, weights, sims, w_rnorm, grad_out, out):
             do(factor_a, t - 1)
             do(one_minus_pooled, t - 1)
             do(constant_term, t - 1)
+            for i in now:
+                for half in range(FEATURE_HALVES):
+                    do(dot, i, half)
             for j in range(AS_PIECES):
                 do(scaled_sims, t - 1, j)
-            if preparing:
-                group_wn(t, 1)
+                if j == 0:
+                    for i in now:
+                        do(coefficient, i)
             for i in before:
                 for half in range(FEATURE_HALVES):
-                    do(project, i, half)
-            if preparing:
-                quantise_wn(t)
-                if t + 2 < CLASS_TILES:
-                    load_weights(t + 2)
-            for i in now:
-                for half in range(FEATURE_HALVES):
-                    do(mx_matmuls, i, half)
-            for j in range(pieces_of(t + 1)):
-                do(maximum, t + 1, j)
-            for i in now:
-                do(dot, i, 0)
+                    do(divide_by_nx, i, half)
+                do(store, i)
             for u in range(CLASS_TILES):
                 do(bracket, t - 2, u)
                 do(gradient, t - 2, u)
@@ -389,18 +383,16 @@ def tile_lsc_t_v_kernel(tc, x, weights, sims, w_rnorm, grad_out, out):
             do(recip_z, t)
             for u in range(CLASS_TILES):
                 do(shifted, t + 1, u)
-            for i in before:
-                for half in range(FEATURE_HALVES):
-                    do(divide_by_nx, i, half)
-                do(store, i)
             do(norms, t - MX_LAG + 1)
-            for i in now:
-                do(dot, i, 1)
+            for j in range(pieces_of(t + 2)):
+                do(maximum, t + 2, j)
             do(quantise, t - 2)
-            for i in now:
-                do(coefficient, i)
-            if 0 <= t + 1 < CLASS_TILES:
+            if preparing:
                 scale_wn(t + 1)
                 group_wn(t + 1, 0)
+                group_wn(t + 1, 1)
+                quantise_wn(t + 1)
+                if t + 3 < CLASS_TILES:
+                    load_weights(t + 3)
             do(load_sims, t + 4)
             do(load_x, t)

@@ -34,6 +34,7 @@ SCALE_ON_SCALAR = (0, 1)
 GROUP_ON = ("vector", "vector")
 FIRST_PIECES = 4
 WARM_TABLE = True
+GROUPED_BY_GPSIMD = (0, 1)
 
 def tile_lsc_t_v_kernel(tc, x, weights, sims, w_rnorm, grad_out, out):
     nc = tc.nc
@@ -109,7 +110,9 @@ def tile_lsc_t_v_kernel(tc, x, weights, sims, w_rnorm, grad_out, out):
         def group_wn(u, half):
             dst = tiles["grouped", u][:, half_cols(half), :].rearrange("c (n i) p -> c n p i", i=4)
             src = tiles["scaled", u][:, :, half_cols(half)].rearrange("c p (n i) -> c n p i", i=4)
-            if GROUP_ON[half] == "scalar":
+            if u in GROUPED_BY_GPSIMD:
+                nc.gpsimd.tensor_scalar(out=dst, in0=src, scalar1=1.0, scalar2=0.0, op0=ALU.mult, op1=ALU.add)
+            elif GROUP_ON[half] == "scalar":
                 nc.scalar.copy(out=dst, in_=src)
             elif GROUP_ON[half] == "gpsimd":
                 nc.gpsimd.tensor_scalar(out=dst, in0=src, scalar1=1.0, scalar2=0.0, op0=ALU.mult, op1=ALU.add)
@@ -388,10 +391,13 @@ def tile_lsc_t_v_kernel(tc, x, weights, sims, w_rnorm, grad_out, out):
                 do(maximum, t + 2, j)
             do(quantise, t - 2)
             if preparing:
+                if t in GROUPED_BY_GPSIMD:
+                    quantise_wn(t)
                 scale_wn(t + 1)
                 group_wn(t + 1, 0)
                 group_wn(t + 1, 1)
-                quantise_wn(t + 1)
+                if t + 1 not in GROUPED_BY_GPSIMD:
+                    quantise_wn(t + 1)
                 if t + 3 < CLASS_TILES:
                     load_weights(t + 3)
             do(load_sims, t + 4)

@@ -361,6 +361,12 @@ def tile_lsc_t_v_kernel(tc, x, weights, sims, w_rnorm, grad_out, out):
                 do(exponential, t, u)
                 do(weighted, t, u)
                 do(proxy_sums, t, u)
+            if t == 0:
+                maximum(1, 0)
+                quantise_wn(0)
+                scale_wn(1)
+                group_wn(1, 0)
+                group_wn(1, 1)
             for j in range(pieces_of(t + 1)):
                 do(split, t + 1, j)
             do(square_x, t - MX_LAG + 1)
@@ -387,15 +393,17 @@ def tile_lsc_t_v_kernel(tc, x, weights, sims, w_rnorm, grad_out, out):
             for u in range(CLASS_TILES):
                 do(shifted, t + 1, u)
             do(norms, t - MX_LAG + 1)
-            for j in range(pieces_of(t + 2)):
-                do(maximum, t + 2, j)
+            if t >= 0:
+                for j in range(pieces_of(t + 2)):
+                    do(maximum, t + 2, j)
             do(quantise, t - 2)
             if preparing:
-                if t in GROUPED_BY_GPSIMD:
-                    quantise_wn(t)
-                scale_wn(t + 1)
-                group_wn(t + 1, 0)
-                group_wn(t + 1, 1)
+                if t == 1:
+                    quantise_wn(1)
+                if t != 0:
+                    scale_wn(t + 1)
+                    group_wn(t + 1, 0)
+                    group_wn(t + 1, 1)
                 if t + 1 not in GROUPED_BY_GPSIMD:
                     quantise_wn(t + 1)
                 if t + 3 < CLASS_TILES:

@@ -235,6 +235,14 @@ def tile_lsc_t_v_kernel(tc, x, weights, sims, w_rnorm, grad_out, out):
                 in1=tiles["a", i][:, cols].unsqueeze(1).to_broadcast([P, PROXIES, n]), op=ALU.mult,
             )
 
+        def scaled_sims_of(i, u):
+            if u == 0:
+                tiles["a_sims", i] = big.tile([P, PROXIES, CLASSES], F32, name="a_sims", bufs=AS_BUFS)
+            nc.gpsimd.tensor_tensor(
+                out=tiles["a_sims", i][:, :, block(u)], in0=tiles["planes", i][:, :, block(u)],
+                in1=tiles["a", i][:, block(u)].unsqueeze(1).to_broadcast([P, PROXIES, P]), op=ALU.mult,
+            )
+
         def bracket(i, u):
             tiles["h_t", i, u] = transposed_sum(tiles["a_sims", i], tiles["a_const", i], u)
 
@@ -249,13 +257,22 @@ def tile_lsc_t_v_kernel(tc, x, weights, sims, w_rnorm, grad_out, out):
             )
 
         def quantise(i):
-            d_codes = small.tile([P, CLASS_TILES * P], U32, bufs=CODE_BUFS, align_bytes=64)
-            d_scales = small.tile([P, CLASS_TILES * P], U8, bufs=CODE_BUFS, align_bytes=64)
+            d_codes = small.tile([P, CLASS_TILES * P], U32, name="d_codes", bufs=CODE_BUFS, align_bytes=64)
+            d_scales = small.tile([P, CLASS_TILES * P], U8, name="d_scales", bufs=CODE_BUFS, align_bytes=64)
             nc.vector.quantize_mx(
                 out=d_codes[:].bitcast(E5M2X4), scales=d_scales[:],
                 in_=tiles["dsims", i][:].rearrange("c u b p -> c (u b p)"),
             )
             tiles["codes", i], tiles["scales", i] = d_codes, d_scales
+
+        def quantise_of(i, u):
+            if u == 0:
+                tiles["codes", i] = small.tile([P, CLASS_TILES * P], U32, name="d_codes", bufs=CODE_BUFS, align_bytes=64)
+                tiles["scales", i] = small.tile([P, CLASS_TILES * P], U8, name="d_scales", bufs=CODE_BUFS, align_bytes=64)
+            nc.vector.quantize_mx(
+                out=tiles["codes", i][:, block(u)].bitcast(E5M2X4), scales=tiles["scales", i][:, block(u)],
+                in_=tiles["dsims", i][:, u].rearrange("c b p -> c (b p)"),
+            )
 
         def square_x(i):
             nx2 = outs.tile([P, 1], F32, bufs=4)
@@ -279,6 +296,19 @@ def tile_lsc_t_v_kernel(tc, x, weights, sims, w_rnorm, grad_out, out):
             for u in range(CLASS_TILES):
                 nc.tensor.matmul_mx(
                     out=acc[:],
+                    lhsT=tiles["codes", i][:, block(u)].bitcast(E5M2X4),
+                    lhsT_scale=tiles["scales", i][:, block(u)],
+                    rhs=w_codes[:, u, half_cols(half)].bitcast(E4M3X4),
+                    rhs_scale=w_scales[:, u, half_cols(half)],
+                    start=(u == 0), stop=(u == CLASS_TILES - 1),
+                )
+
+        def mx_matmuls_of(i, u):
+            for half in range(FEATURE_HALVES):
+                if u == 0:
+                    tiles["acc", i, half] = psum_1.tile([P, N_MOVING], F32, name="sums")
+                nc.tensor.matmul_mx(
+                    out=tiles["acc", i, half][:],
                     lhsT=tiles["codes", i][:, block(u)].bitcast(E5M2X4),
                     lhsT_scale=tiles["scales", i][:, block(u)],
                     rhs=w_codes[:, u, half_cols(half)].bitcast(E4M3X4),
@@ -330,6 +360,15 @@ def tile_lsc_t_v_kernel(tc, x, weights, sims, w_rnorm, grad_out, out):
         def store(i):
             nc.sync.dma_start(out=out[i * P : (i + 1) * P, :], in_=tiles["y", i][:])
 
+        def store_half(i, half):
+            nc.sync.dma_start(
+                out=out[i * P : (i + 1) * P, half_cols(half)], in_=tiles["y", i][:, half_cols(half)]
+            )
+
+        def both(fn, i):
+            for half in range(FEATURE_HALVES):
+                fn(i, half)
+
         def do(fn, i, *args):
             if 0 <= i < TOKEN_TILES:
                 fn(i, *args)
@@ -347,7 +386,7 @@ def tile_lsc_t_v_kernel(tc, x, weights, sims, w_rnorm, grad_out, out):
         load_sims(2)
         for j in range(pieces_of(0)):
             maximum(0, j)
-        for t in range(-1, TOKEN_TILES + MX_LAG + 1):
+        for t in range(-1, TOKEN_TILES):
             now, before = matmul_tiles(t), matmul_tiles(t - 1)
             preparing = 0 <= t + 1 < CLASS_TILES
             for i in before:
@@ -369,7 +408,8 @@ def tile_lsc_t_v_kernel(tc, x, weights, sims, w_rnorm, grad_out, out):
                 group_wn(1, 1)
             for j in range(pieces_of(t + 1)):
                 do(split, t + 1, j)
-            do(square_x, t - MX_LAG + 1)
+            if t < TOKEN_TILES - 1:
+                do(square_x, t - MX_LAG + 1)
             do(factor_a, t - 1)
             do(one_minus_pooled, t - 1)
             do(constant_term, t - 1)
@@ -382,9 +422,13 @@ def tile_lsc_t_v_kernel(tc, x, weights, sims, w_rnorm, grad_out, out):
                     for i in now:
                         do(coefficient, i)
             for i in before:
-                for half in range(FEATURE_HALVES):
-                    do(divide_by_nx, i, half)
-                do(store, i)
+                if t < TOKEN_TILES - 1:
+                    for half in range(FEATURE_HALVES):
+                        do(divide_by_nx, i, half)
+                    do(store, i)
+            if t >= 0:
+                for j in range(pieces_of(t + 2)):
+                    do(maximum, t + 2, j)
             for u in range(CLASS_TILES):
                 do(bracket, t - 2, u)
                 do(gradient, t - 2, u)
@@ -392,10 +436,8 @@ def tile_lsc_t_v_kernel(tc, x, weights, sims, w_rnorm, grad_out, out):
             do(recip_z, t)
             for u in range(CLASS_TILES):
                 do(shifted, t + 1, u)
-            do(norms, t - MX_LAG + 1)
-            if t >= 0:
-                for j in range(pieces_of(t + 2)):
-                    do(maximum, t + 2, j)
+            if t < TOKEN_TILES - 1:
+                do(norms, t - MX_LAG + 1)
             do(quantise, t - 2)
             if preparing:
                 if t == 1:
@@ -403,10 +445,71 @@ def tile_lsc_t_v_kernel(tc, x, weights, sims, w_rnorm, grad_out, out):
                 if t != 0:
                     scale_wn(t + 1)
                     group_wn(t + 1, 0)
-                    group_wn(t + 1, 1)
-                if t + 1 not in GROUPED_BY_GPSIMD:
+                    if t + 1 < CLASS_TILES - 1:
+                        group_wn(t + 1, 1)
+                if t + 1 not in GROUPED_BY_GPSIMD and t + 1 < CLASS_TILES - 1:
                     quantise_wn(t + 1)
                 if t + 3 < CLASS_TILES:
                     load_weights(t + 3)
+            if t == CLASS_TILES - 1:
+                group_wn(t, 1)
+                quantise_wn(t)
             do(load_sims, t + 4)
             do(load_x, t)
+
+        last = TOKEN_TILES - 1
+        factor_a(last)
+        one_minus_q(last)
+        one_minus_pooled(last)
+        constant_term(last)
+        both(project, last - 4)
+        for u in range(CLASS_TILES):
+            bracket(last - 1, u)
+            gradient(last - 1, u)
+        square_x(last - 3)
+        both(divide_by_nx, last - 5)
+        store(last - 5)
+        for i in (last - 2, last - 1, last):
+            square_x(i)
+        both(mx_matmuls, last - 3)
+        both(mx_matmuls, last - 2)
+        both(divide_by_nx, last - 4)
+        store(last - 4)
+        quantise(last - 1)
+        both(dot, last - 3)
+        both(dot, last - 2)
+        scaled_sims_of(last, 0)
+        norms(last - 3)
+        norms(last - 2)
+        coefficient(last - 3)
+        coefficient(last - 2)
+        for u in range(1, CLASS_TILES):
+            scaled_sims_of(last, u)
+        norms(last - 1)
+        norms(last)
+        both(project, last - 3)
+        both(project, last - 2)
+        both(mx_matmuls, last - 1)
+        for i in (last - 3, last - 2):
+            both(divide_by_nx, i)
+            store(i)
+        both(dot, last - 1)
+        coefficient(last - 1)
+        for u in range(CLASS_TILES):
+            bracket(last, u)
+        for u in range(CLASS_TILES):
+            gradient(last, u)
+            if u > 0:
+                quantise_of(last, u - 1)
+        both(project, last - 1)
+        quantise_of(last, CLASS_TILES - 1)
+        for u in range(CLASS_TILES):
+            mx_matmuls_of(last, u)
+        both(divide_by_nx, last - 1)
+        store(last - 1)
+        both(dot, last)
+        coefficient(last)
+        for half in range(FEATURE_HALVES):
+            project(last, half)
+            divide_by_nx(last, half)
+            store_half(last, half)

from contextlib import ExitStack

import concourse.mybir as mybir
from concourse.masks import make_identity

F32 = mybir.dt.float32
BF16 = mybir.dt.bfloat16
U32 = mybir.dt.uint32
U8 = mybir.dt.uint8
E4M3X4 = mybir.dt.float8_e4m3fn_x4
E5M2X4 = mybir.dt.float8_e5m2_x4
ALU = mybir.AluOpType
ACT = mybir.ActivationFunctionType
AXIS = mybir.AxisListType

P = 128
TOKENS = 2048
FEATURES = 1024
CLASSES = 512
PROXIES = 4
TOKEN_TILES = TOKENS // P
CLASS_TILES = CLASSES // P
N_MOVING = 512
FEATURE_HALVES = FEATURES // N_MOVING

FLOPS = 2 * TOKENS * CLASSES * PROXIES * FEATURES


AS_PIECES = 2
AS_BUFS = 2
CODE_BUFS = 5
MX_LAG = 4
SCALE_ON_SCALAR = (0, 1)
GROUP_ON = ("vector", "vector")
FIRST_PIECES = 4
WARM_TABLE = True
GROUPED_BY_GPSIMD = (0, 1)

def tile_lsc_t_v_kernel(tc, x, weights, sims, w_rnorm, grad_out, out):
    nc = tc.nc
    with ExitStack() as ctx:
        consts = ctx.enter_context(tc.tile_pool(name="consts", bufs=1))
        wprep = ctx.enter_context(tc.tile_pool(name="wprep", bufs=1))
        loads = ctx.enter_context(tc.tile_pool(name="loads", bufs=3))
        big = ctx.enter_context(tc.tile_pool(name="big", bufs=2))
        small = ctx.enter_context(tc.tile_pool(name="small", bufs=2))
        outs = ctx.enter_context(tc.tile_pool(name="outs", bufs=2))
        psum_w = ctx.enter_context(tc.psum_pool(name="psum_w", bufs=4))
        psum_1 = ctx.enter_context(tc.psum_pool(name="psum_1", bufs=4))
        ctx.enter_context(tc.manual_schedule())

        ident = consts.tile([P, P], F32)
        make_identity(nc, ident[:])
        rnorm = consts.tile([P, CLASS_TILES, PROXIES], F32)
        w_codes = consts.tile([P, CLASS_TILES, FEATURES], U32, align_bytes=64)
        w_scales = consts.tile([P, CLASS_TILES, FEATURES], U8, align_bytes=64)

        exponents = consts.tile([P, 2], F32)
        nc.gpsimd.memset(exponents[:, 0:1], -0.5)
        nc.gpsimd.memset(exponents[:, 1:2], -1.0)

        tiles = {}

        if WARM_TABLE:
            warm = consts.tile([P, 1], F32)
            nc.scalar.activation(out=warm[:], in_=exponents[:, 0:1], func=ACT.Exp)

        def pieces_of(i):
            return FIRST_PIECES if i == 0 else 1

        def block(u):
            return slice(u * P, (u + 1) * P)

        def half_cols(half):
            return slice(half * N_MOVING, (half + 1) * N_MOVING)

        def load_sims(i):
            rows = slice(i * P, (i + 1) * P)
            s_sb = loads.tile([P, CLASSES * PROXIES], F32)
            n = CLASSES * PROXIES // pieces_of(i)
            for j in range(pieces_of(i)):
                nc.sync.dma_start(out=s_sb[:, j * n : (j + 1) * n], in_=sims[rows, j * n : (j + 1) * n])
            g_sb = loads.tile([P, CLASSES], BF16, bufs=6)
            nc.sync.dma_start(out=g_sb[:], in_=grad_out[rows, :])
            tiles["s", i], tiles["g", i] = s_sb, g_sb

        def load_x(i):
            x_sb = loads.tile([P, FEATURES], BF16, bufs=7)
            nc.sync.dma_start(out=x_sb[:], in_=x[i * P : (i + 1) * P, :])
            tiles["x", i] = x_sb

        def load_weights(u):
            raw = wprep.tile([P, PROXIES, FEATURES], BF16, bufs=2)
            nc.sync.dma_start(
                out=raw[:],
                in_=weights[u * P : (u + 1) * P, :].rearrange("c (p d) -> c p d", p=PROXIES),
            )
            tiles["raw", u] = raw

        def scale_wn(u):
            scaled = wprep.tile([P, PROXIES, FEATURES], BF16)
            for p in range(PROXIES):
                nc.vector.tensor_scalar(
                    out=scaled[:, p, :], in0=tiles["raw", u][:, p, :],
                    scalar1=rnorm[:, u, p : p + 1], scalar2=None, op0=ALU.mult,
                )
            tiles["scaled", u] = scaled
            tiles["grouped", u] = wprep.tile([P, FEATURES, PROXIES], BF16, name="grouped", align_bytes=64)

        def group_wn(u, half):
            dst = tiles["grouped", u][:, half_cols(half), :].rearrange("c (n i) p -> c n p i", i=4)
            src = tiles["scaled", u][:, :, half_cols(half)].rearrange("c p (n i) -> c n p i", i=4)
            if u in GROUPED_BY_GPSIMD:
                nc.gpsimd.tensor_scalar(out=dst, in0=src, scalar1=1.0, scalar2=0.0, op0=ALU.mult, op1=ALU.add)
            elif GROUP_ON[half] == "scalar":
                nc.scalar.copy(out=dst, in_=src)
            elif GROUP_ON[half] == "gpsimd":
                nc.gpsimd.tensor_scalar(out=dst, in0=src, scalar1=1.0, scalar2=0.0, op0=ALU.mult, op1=ALU.add)
            else:
                nc.vector.tensor_copy(out=dst, in_=src)

        def quantise_wn(u):
            nc.vector.quantize_mx(
                out=w_codes[:, u, :].bitcast(E4M3X4), scales=w_scales[:, u, :],
                in_=tiles["grouped", u][:].rearrange("c d p -> c (d p)"),
            )

        def split(i, j):
            if j == 0:
                tiles["planes", i] = big.tile([P, PROXIES, CLASSES], F32, name="planes", bufs=3)
            n = CLASSES // pieces_of(i)
            nc.scalar.copy(
                out=tiles["planes", i][:, :, j * n : (j + 1) * n].rearrange("b p c -> b c p"),
                in_=tiles["s", i][:, j * n * PROXIES : (j + 1) * n * PROXIES].rearrange(
                    "b (c p) -> b c p", p=PROXIES
                ),
            )

        def maximum(i, j):
            if j == 0:
                tiles["neg_m", i] = small.tile([P, CLASSES], F32, name="neg_m", bufs=5)
            n = CLASSES // pieces_of(i)
            nc.vector.tensor_reduce(
                out=tiles["neg_m", i][:, j * n : (j + 1) * n],
                in_=tiles["s", i][:, j * n * PROXIES : (j + 1) * n * PROXIES].rearrange(
                    "b (c p) -> b c p", p=PROXIES
                ),
                axis=AXIS.X, op=ALU.max, negate=True,
            )

        def transposed_sum(full, per_class, u):
            bank = psum_w.tile([P, PROXIES, P], F32)
            for p in range(PROXIES):
                nc.tensor.matmul(
                    out=bank[:, p, :], lhsT=full[:, p, block(u)], rhs=ident[:],
                    is_transpose=True, start=True, stop=False,
                )
                nc.tensor.matmul(
                    out=bank[:, p, :], lhsT=per_class[:, block(u)], rhs=ident[:],
                    is_transpose=True, start=False, stop=True,
                )
            return bank

        def shifted(i, u):
            tiles["d_t", i, u] = transposed_sum(tiles["planes", i], tiles["neg_m", i], u)

        def exponential(i, u):
            if u == 0:
                tiles["e", i] = big.tile([P, CLASS_TILES, PROXIES, P], F32, name="e", bufs=3)
            nc.scalar.activation(out=tiles["e", i][:, u], in_=tiles["d_t", i, u][:], func=ACT.Exp)

        def weighted(i, u):
            if u == 0:
                tiles["f", i] = big.tile([P, CLASS_TILES, PROXIES, P], F32, name="f", bufs=1)
            nc.vector.scalar_tensor_tensor(
                out=tiles["f", i][:, u], in0=tiles["d_t", i, u][:], scalar=-1.0,
                in1=tiles["e", i][:, u], op0=ALU.add, op1=ALU.mult,
            )

        def proxy_sums(i, u):
            if u == 0:
                tiles["z", i] = psum_1.tile([P, CLASSES], F32, name="sums")
                tiles["fs", i] = psum_1.tile([P, CLASSES], F32, name="sums")
            for src, dst in ((tiles["e", i], tiles["z", i]), (tiles["f", i], tiles["fs", i])):
                for p in range(PROXIES):
                    nc.tensor.matmul(
                        out=dst[:, block(u)], lhsT=src[:, u, p, :], rhs=ident[:],
                        is_transpose=True, start=(p == 0), stop=(p == PROXIES - 1),
                    )

        def log_z(i):
            ln_z = small.tile([P, CLASSES], F32, bufs=1)
            nc.scalar.activation(out=ln_z[:], in_=tiles["z", i][:], func=ACT.Ln)
            tiles["ln_z", i] = ln_z

        def recip_z(i):
            rz = small.tile([P, CLASSES], F32)
            nc.scalar.activation(out=rz[:], in_=tiles["ln_z", i][:], func=ACT.Exp, scale=-1.0)
            tiles["rz", i] = rz

        def one_minus_q(i):
            one_q = small.tile([P, CLASSES], F32, bufs=1)
            nc.vector.scalar_tensor_tensor(
                out=one_q[:], in0=tiles["fs", i][:], scalar=-1.0, in1=tiles["rz", i][:],
                op0=ALU.mult, op1=ALU.mult,
            )
            tiles["one_q", i] = one_q

        def factor_a(i):
            a = small.tile([P, CLASSES], F32)
            nc.gpsimd.tensor_tensor(out=a[:], in0=tiles["g", i][:], in1=tiles["rz", i][:], op=ALU.mult)
            tiles["a", i] = a

        def one_minus_pooled(i):
            one_pooled = small.tile([P, CLASSES], F32, bufs=1)
            nc.gpsimd.tensor_tensor(
                out=one_pooled[:], in0=tiles["neg_m", i][:], in1=tiles["one_q", i][:], op=ALU.add
            )
            tiles["one_pooled", i] = one_pooled

        def constant_term(i):
            a_const = small.tile([P, CLASSES], F32)
            nc.gpsimd.tensor_tensor(
                out=a_const[:], in0=tiles["a", i][:], in1=tiles["one_pooled", i][:], op=ALU.mult
            )
            tiles["a_const", i] = a_const

        def scaled_sims(i, j):
            if j == 0:
                tiles["a_sims", i] = big.tile([P, PROXIES, CLASSES], F32, name="a_sims", bufs=AS_BUFS)
            n = CLASSES // AS_PIECES
            cols = slice(j * n, (j + 1) * n)
            nc.gpsimd.tensor_tensor(
                out=tiles["a_sims", i][:, :, cols], in0=tiles["planes", i][:, :, cols],
                in1=tiles["a", i][:, cols].unsqueeze(1).to_broadcast([P, PROXIES, n]), op=ALU.mult,
            )

        def scaled_sims_of(i, u):
            if u == 0:
                tiles["a_sims", i] = big.tile([P, PROXIES, CLASSES], F32, name="a_sims", bufs=AS_BUFS)
            nc.gpsimd.tensor_tensor(
                out=tiles["a_sims", i][:, :, block(u)], in0=tiles["planes", i][:, :, block(u)],
                in1=tiles["a", i][:, block(u)].unsqueeze(1).to_broadcast([P, PROXIES, P]), op=ALU.mult,
            )

        def bracket(i, u):
            tiles["h_t", i, u] = transposed_sum(tiles["a_sims", i], tiles["a_const", i], u)

        def gradient(i, u):
            if u == 0:
                tiles["dsims", i] = big.tile(
                    [P, CLASS_TILES, P, PROXIES], BF16, name="dsims", bufs=1, align_bytes=64
                )
            nc.vector.tensor_tensor(
                out=tiles["dsims", i][:, u], in0=tiles["h_t", i, u][:].rearrange("c p b -> c b p"),
                in1=tiles["e", i][:, u].rearrange("c p b -> c b p"), op=ALU.mult,
            )

        def quantise(i):
            d_codes = small.tile([P, CLASS_TILES * P], U32, name="d_codes", bufs=CODE_BUFS, align_bytes=64)
            d_scales = small.tile([P, CLASS_TILES * P], U8, name="d_scales", bufs=CODE_BUFS, align_bytes=64)
            nc.vector.quantize_mx(
                out=d_codes[:].bitcast(E5M2X4), scales=d_scales[:],
                in_=tiles["dsims", i][:].rearrange("c u b p -> c (u b p)"),
            )
            tiles["codes", i], tiles["scales", i] = d_codes, d_scales

        def quantise_of(i, u):
            if u == 0:
                tiles["codes", i] = small.tile([P, CLASS_TILES * P], U32, name="d_codes", bufs=CODE_BUFS, align_bytes=64)
                tiles["scales", i] = small.tile([P, CLASS_TILES * P], U8, name="d_scales", bufs=CODE_BUFS, align_bytes=64)
            nc.vector.quantize_mx(
                out=tiles["codes", i][:, block(u)].bitcast(E5M2X4), scales=tiles["scales", i][:, block(u)],
                in_=tiles["dsims", i][:, u].rearrange("c b p -> c (b p)"),
            )

        def square_x(i):
            nx2 = outs.tile([P, 1], F32, bufs=4)
            x_sq = outs.tile([P, FEATURES], BF16, bufs=1)
            nc.scalar.activation(
                out=x_sq[:], in_=tiles["x", i][:], func=ACT.Square, accum_out=nx2[:]
            )
            tiles["nx2", i] = nx2

        def norms(i):
            inv_nx = outs.tile([P, 2], F32, bufs=4)
            nc.gpsimd.tensor_tensor(
                out=inv_nx[:], in0=tiles["nx2", i][:].to_broadcast([P, 2]), in1=exponents[:],
                op=ALU.pow,
            )
            tiles["inv_nx", i] = inv_nx

        def mx_matmuls(i, half):
            acc = psum_1.tile([P, N_MOVING], F32, name="sums")
            tiles["acc", i, half] = acc
            for u in range(CLASS_TILES):
                nc.tensor.matmul_mx(
                    out=acc[:],
                    lhsT=tiles["codes", i][:, block(u)].bitcast(E5M2X4),
                    lhsT_scale=tiles["scales", i][:, block(u)],
                    rhs=w_codes[:, u, half_cols(half)].bitcast(E4M3X4),
                    rhs_scale=w_scales[:, u, half_cols(half)],
                    start=(u == 0), stop=(u == CLASS_TILES - 1),
                )

        def mx_matmuls_of(i, u):
            for half in range(FEATURE_HALVES):
                if u == 0:
                    tiles["acc", i, half] = psum_1.tile([P, N_MOVING], F32, name="sums")
                nc.tensor.matmul_mx(
                    out=tiles["acc", i, half][:],
                    lhsT=tiles["codes", i][:, block(u)].bitcast(E5M2X4),
                    lhsT_scale=tiles["scales", i][:, block(u)],
                    rhs=w_codes[:, u, half_cols(half)].bitcast(E4M3X4),
                    rhs_scale=w_scales[:, u, half_cols(half)],
                    start=(u == 0), stop=(u == CLASS_TILES - 1),
                )

        def dot(i, half):
            if half == 0:
                tiles["dots", i] = outs.tile([P, FEATURE_HALVES], F32, name="dots")
            products = outs.tile([P, N_MOVING], F32, bufs=1)
            nc.vector.scalar_tensor_tensor(
                out=products[:], in0=tiles["acc", i, half][:], scalar=-1.0,
                in1=tiles["x", i][:, half_cols(half)], op0=ALU.mult, op1=ALU.mult,
                accum_out=tiles["dots", i][:, half : half + 1],
            )

        def coefficient(i):
            neg_c = outs.tile([P, 1], F32)
            nc.gpsimd.tensor_scalar(
                out=neg_c[:], in0=tiles["dots", i][:, 0:1], scalar1=tiles["dots", i][:, 1:2],
                scalar2=tiles["inv_nx", i][:, 1:2], op0=ALU.add, op1=ALU.mult,
            )
            tiles["neg_c", i] = neg_c

        def project(i, half):
            if half == 0:
                tiles["zed", i] = outs.tile([P, FEATURES], F32, name="zed", bufs=1)
            nc.vector.scalar_tensor_tensor(
                out=tiles["zed", i][:, half_cols(half)], in0=tiles["x", i][:, half_cols(half)],
                scalar=tiles["neg_c", i][:, 0:1], in1=tiles["acc", i, half][:],
                op0=ALU.mult, op1=ALU.add,
            )

        def divide_by_nx(i, half):
            if half == 0:
                tiles["y", i] = outs.tile([P, FEATURES], F32, name="y")
            if half in SCALE_ON_SCALAR:
                nc.scalar.activation(
                    out=tiles["y", i][:, half_cols(half)], in_=tiles["zed", i][:, half_cols(half)],
                    func=ACT.Copy, scale=tiles["inv_nx", i][:, 0:1],
                )
            else:
                nc.gpsimd.tensor_scalar(
                    out=tiles["y", i][:, half_cols(half)], in0=tiles["zed", i][:, half_cols(half)],
                    scalar1=tiles["inv_nx", i][:, 0:1], scalar2=0.0, op0=ALU.mult, op1=ALU.add,
                )

        def store(i):
            nc.sync.dma_start(out=out[i * P : (i + 1) * P, :], in_=tiles["y", i][:])

        def store_half(i, half):
            nc.sync.dma_start(
                out=out[i * P : (i + 1) * P, half_cols(half)], in_=tiles["y", i][:, half_cols(half)]
            )

        def both(fn, i):
            for half in range(FEATURE_HALVES):
                fn(i, half)

        def do(fn, i, *args):
            if 0 <= i < TOKEN_TILES:
                fn(i, *args)

        def matmul_tiles(t):
            return [t - MX_LAG] if 0 <= t - MX_LAG < TOKEN_TILES else []

        load_sims(0)
        nc.sync.dma_start(
            out=rnorm[:], in_=w_rnorm.rearrange("(u c p) -> c u p", u=CLASS_TILES, p=PROXIES)
        )
        load_weights(0)
        load_sims(1)
        load_weights(1)
        load_sims(2)
        for j in range(pieces_of(0)):
            maximum(0, j)
        for t in range(-1, TOKEN_TILES):
            now, before = matmul_tiles(t), matmul_tiles(t - 1)
            preparing = 0 <= t + 1 < CLASS_TILES
            for i in before:
                for half in range(FEATURE_HALVES):
                    do(project, i, half)
            for i in now:
                for half in range(FEATURE_HALVES):
                    do(mx_matmuls, i, half)
            do(one_minus_q, t - 1)
            for u in range(CLASS_TILES):
                do(exponential, t, u)
                do(weighted, t, u)
                do(proxy_sums, t, u)
            if t == 0:
                maximum(1, 0)
                quantise_wn(0)
                scale_wn(1)
                group_wn(1, 0)
                group_wn(1, 1)
            for j in range(pieces_of(t + 1)):
                do(split, t + 1, j)
            if t < TOKEN_TILES - 1:
                do(square_x, t - MX_LAG + 1)
            do(factor_a, t - 1)
            do(one_minus_pooled, t - 1)
            do(constant_term, t - 1)
            for i in now:
                for half in range(FEATURE_HALVES):
                    do(dot, i, half)
            for j in range(AS_PIECES):
                do(scaled_sims, t - 1, j)
                if j == 0:
                    for i in now:
                        do(coefficient, i)
            for i in before:
                if t < TOKEN_TILES - 1:
                    for half in range(FEATURE_HALVES):
                        do(divide_by_nx, i, half)
                    do(store, i)
            if t >= 0:
                for j in range(pieces_of(t + 2)):
                    do(maximum, t + 2, j)
            for u in range(CLASS_TILES):
                do(bracket, t - 2, u)
                do(gradient, t - 2, u)
            do(log_z, t)
            do(recip_z, t)
            for u in range(CLASS_TILES):
                do(shifted, t + 1, u)
            if t < TOKEN_TILES - 1:
                do(norms, t - MX_LAG + 1)
            do(quantise, t - 2)
            if preparing:
                if t == 1:
                    quantise_wn(1)
                if t != 0:
                    scale_wn(t + 1)
                    group_wn(t + 1, 0)
                    if t + 1 < CLASS_TILES - 1:
                        group_wn(t + 1, 1)
                if t + 1 not in GROUPED_BY_GPSIMD and t + 1 < CLASS_TILES - 1:
                    quantise_wn(t + 1)
                if t + 3 < CLASS_TILES:
                    load_weights(t + 3)
            if t == CLASS_TILES - 1:
                group_wn(t, 1)
                quantise_wn(t)
            do(load_sims, t + 4)
            do(load_x, t)

        last = TOKEN_TILES - 1
        factor_a(last)
        one_minus_q(last)
        one_minus_pooled(last)
        constant_term(last)
        both(project, last - 4)
        for u in range(CLASS_TILES):
            bracket(last - 1, u)
            gradient(last - 1, u)
        square_x(last - 3)
        both(divide_by_nx, last - 5)
        store(last - 5)
        for i in (last - 2, last - 1, last):
            square_x(i)
        both(mx_matmuls, last - 3)
        both(mx_matmuls, last - 2)
        both(divide_by_nx, last - 4)
        store(last - 4)
        quantise(last - 1)
        both(dot, last - 3)
        both(dot, last - 2)
        scaled_sims_of(last, 0)
        norms(last - 3)
        norms(last - 2)
        coefficient(last - 3)
        coefficient(last - 2)
        for u in range(1, CLASS_TILES):
            scaled_sims_of(last, u)
        norms(last - 1)
        norms(last)
        both(project, last - 3)
        both(project, last - 2)
        both(mx_matmuls, last - 1)
        for i in (last - 3, last - 2):
            both(divide_by_nx, i)
            store(i)
        both(dot, last - 1)
        coefficient(last - 1)
        for u in range(CLASS_TILES):
            bracket(last, u)
        for u in range(CLASS_TILES):
            gradient(last, u)
            if u > 0:
                quantise_of(last, u - 1)
        both(project, last - 1)
        quantise_of(last, CLASS_TILES - 1)
        for u in range(CLASS_TILES):
            mx_matmuls_of(last, u)
        both(divide_by_nx, last - 1)
        store(last - 1)
        both(dot, last)
        coefficient(last)
        for half in range(FEATURE_HALVES):
            project(last, half)
            divide_by_nx(last, half)
            store_half(last, half)
